import numpy as np
import ml_dtypes


def mxq(x, axis, fmt="e4m3"):
    dtype, down = {"e4m3": (ml_dtypes.float8_e4m3fn, 7), "e5m2": (ml_dtypes.float8_e5m2, 14)}[fmt]
    v = np.moveaxis(np.asarray(x, np.float32).astype(ml_dtypes.bfloat16).astype(np.float64), axis, -1)
    blocks = v.reshape(v.shape[:-1] + (-1, 32))
    amax = np.abs(blocks).max(-1, keepdims=True)
    byte = np.maximum(np.where(amax > 0, np.frexp(amax)[1] - 1 + 127, 0) - down, 1)
    scale = np.exp2(byte - 127.0)
    codes = (blocks / scale).astype(np.float32).astype(dtype).astype(np.float64)
    return np.moveaxis((codes * scale).reshape(v.shape), -1, axis)


WIDE = False


def mx_kscale(k):
    if not WIDE:
        return np.ones(k)
    levels = np.array([10, -10, 5, -5, 0])
    a = np.random.permutation(np.resize(levels, k // 512 * 4)).reshape(k // 512, 4)
    idx = np.arange(k)
    return np.exp2(a[idx // 512, idx % 128 // 32])


BF16 = ml_dtypes.bfloat16


def bf(x):
    return np.asarray(x, np.float32).astype(BF16)


def f64(x):
    return np.asarray(x).astype(np.float64)


B, N, C, E = 4, 2048, 1024, 256
EPS_SUM = 1e-7
EPS_NORM = 1e-12


def setup_inputs():
    s = mx_kscale(C)
    r = np.random.uniform(0.5, 1.5, (B, N, 1))
    return {"x": bf(np.random.standard_normal((B, N, C)) * r * s),
            "wk": bf(np.random.standard_normal((C, E)) / np.sqrt(C) / s[:, None]),
            "bk": bf(0.3 + 0.3 * np.random.standard_normal(E)),
            "wv": bf(np.random.standard_normal((C, E)) / np.sqrt(C) / s[:, None]),
            "bv": bf(0.1 * np.random.standard_normal(E))}


def reference(x, wk, bk, wv, bv):
    xq = mxq(f64(x), 2, "e4m3")
    k = (xq @ mxq(f64(wk), 0, "e4m3")) + f64(bk)
    v = (xq @ mxq(f64(wv), 0, "e4m3")) + f64(bv)
    k = k - k.mean(axis=2, keepdims=True)
    k2 = k * k
    k2 = k2 / (k2.sum(axis=2, keepdims=True) + EPS_SUM)
    nrm = np.sqrt((k2 * k2).sum(axis=1, keepdims=True))
    k2 = k2 / np.maximum(nrm, EPS_NORM)
    kv = mxq(k2, 1, "e4m3").transpose(0, 2, 1) @ mxq(v, 1, "e4m3")
    return kv, v

@@ -1,0 +1,400 @@
+from contextlib import ExitStack
+
+import concourse.mybir as mybir
+from concourse.masks import make_identity
+
+F32 = mybir.dt.float32
+BF16 = mybir.dt.bfloat16
+U32 = mybir.dt.uint32
+U8 = mybir.dt.uint8
+FP8X4 = mybir.dt.float8_e4m3fn_x4
+ALU = mybir.AluOpType
+ACT = mybir.ActivationFunctionType
+AXIS = mybir.AxisListType
+
+B, N, C, E = 4, 2048, 1024, 256
+EPS_SUM = 1e-7
+EPS_NORM = 1e-12
+FLOPS = 2 * B * N * C * 2 * E + 2 * B * N * E * E
+
+P = 128
+PACK = 4
+K_PASS = P * PACK
+C_PASSES = C // K_PASS
+WORDS = C // 2
+PAIR = 2
+PAIRS_PER_GROUP = PACK // PAIR
+PAIRS_PER_BATCH = N // (PAIR * P)
+GROUPS_PER_BATCH = N // K_PASS
+PAIRS = B * PAIRS_PER_BATCH
+E_BLOCKS = E // P
+
+X_BUFS = 6
+NORM_STEP = PAIRS_PER_BATCH + 4
+LAST_STEP = NORM_STEP + B * PAIRS_PER_BATCH
+
+
+def tile_essattn_pa_t_kernel(tc, x, wk, bk, wv, bv, out_0, out_1):
+    nc = tc.nc
+    x_groups = x.flatten_outer_dims().rearrange("(i p t) c -> i p t c", p=P, t=PACK)
+    v_groups = out_1.flatten_outer_dims().rearrange("(i p t) e -> i p t e", p=P, t=PACK)
+
+    with ExitStack() as ctx:
+        ctx.enter_context(tc.manual_schedule())
+        const = ctx.enter_context(tc.tile_pool(name="const", bufs=1))
+        stream = ctx.enter_context(tc.tile_pool(name="stream", bufs=2))
+        small = ctx.enter_context(tc.tile_pool(name="small", bufs=4))
+        psum = ctx.enter_context(tc.psum_pool(name="psum", bufs=1))
+
+        x_rows, x_t, x_grouped, x_codes, x_scales, acc = {}, {}, {}, {}, {}, {}
+        kb, k_sum, neg_mean, f, f_sum, f_sum_eps, r = {}, {}, {}, {}, {}, {}, {}
+        g_rows, g_t, v_rows, v_grouped = {}, {}, {}, {}
+        norm_parts, norm_sq, norm, r_norm, r_norm_ps, r_norm_rows = {}, {}, {}, {}, {}, {}
+        v_codes, v_scales, k2_grouped, k2_codes, k2_scales, kv_ps = {}, {}, {}, {}, {}, {}
+
+        def load_x(j):
+            if j >= PAIRS:
+                return
+            i, h = divmod(j, PAIRS_PER_GROUP)
+            x_rows[j] = stream.tile([P, PAIR * C], BF16, name="x_rows", tag="x_rows", bufs=X_BUFS)
+            nc.sync.dma_start(
+                out=x_rows[j][:].rearrange("p (t c) -> p t c", t=PAIR),
+                in_=x_groups[i][:, h * PAIR : (h + 1) * PAIR, :],
+            )
+
+        ident = const.tile([P, P], F32)
+        make_identity(nc, ident[:])
+
+        one = const.tile([P, 1], F32)
+        nc.vector.memset(one[:], 1.0)
+        sqrt_one = const.tile([P, 1], F32)
+        nc.scalar.sqrt(sqrt_one[:], one[:])
+
+        w_codes = const.tile([P, C_PASSES, 2 * E], U32, align_bytes=64)
+        w_scales = const.tile([P, C_PASSES, 2 * E], U8, align_bytes=64)
+        with tc.tile_pool(name="w_stage", bufs=1) as w_stage:
+            wk_rows = w_stage.tile([P, C_PASSES * PACK, E], BF16)
+            wv_rows = w_stage.tile([P, C_PASSES * PACK, E], BF16)
+            for rows, w in ((wk_rows, wk), (wv_rows, wv)):
+                nc.sync.dma_start(
+                    out=rows[:].rearrange("p (h e) n -> p h (e n)", e=2),
+                    in_=w.rearrange("(h p e) n -> p h (e n)", p=P, e=2),
+                )
+            for j in range(X_BUFS):
+                load_x(j)
+            w_grouped = w_stage.tile([P, C_PASSES, 2 * E, PACK], BF16, align_bytes=64)
+            for c in range(C_PASSES):
+                for side, rows in enumerate((wk_rows, wv_rows)):
+                    nc.vector.tensor_copy(
+                        out=w_grouped[:, c, side * E : (side + 1) * E, :],
+                        in_=rows[:, c * PACK : (c + 1) * PACK, :].rearrange("p t n -> p n t"),
+                    )
+            for c in range(C_PASSES):
+                nc.vector.quantize_mx(
+                    out=w_codes[:, c, :].bitcast(FP8X4),
+                    scales=w_scales[:, c, :],
+                    in_=w_grouped[:, c].rearrange("p n t -> p (n t)"),
+                )
+
+        bias_bf = const.tile([P, 2 * E], BF16)
+        nc.scalar.dma_start(out=bias_bf[:, 0:E], in_=bk.partition_broadcast(P))
+        nc.scalar.dma_start(out=bias_bf[:, E : 2 * E], in_=bv.partition_broadcast(P))
+        bias = const.tile([P, 2 * E], F32)
+        nc.vector.tensor_copy(out=bias[:], in_=bias_bf[:])
+
+        squares = const.tile([P, PAIR * P], BF16)
+
+        def in_range(j):
+            return 0 <= j < PAIRS
+
+        def transpose_x(j):
+            words = x_rows[j][:].bitcast(F32)
+            x_t[j] = []
+            for t in range(PAIR):
+                bank = psum.tile([P, WORDS // P, P], F32, name="x_t", tag="x_t", bufs=PAIR)
+                for q in range(WORDS // P):
+                    first = t * WORDS + q * P
+                    nc.tensor.transpose(bank[:, q, :], words[:, first : first + P], ident[:])
+                x_t[j].append(bank)
+
+        def regroup_x(j):
+            x_grouped[j] = stream.tile(
+                [P, PAIR * C], BF16, name="x_grouped", tag="x_grouped", align_bytes=64
+            )
+            words = x_grouped[j][:].bitcast(F32)
+            for t in range(PAIR):
+                nc.scalar.copy(
+                    out=words[:, t * WORDS : (t + 1) * WORDS].rearrange(
+                        "p (c r u) -> p c r u", c=C_PASSES, u=2
+                    ),
+                    in_=x_t[j][t][:].rearrange("p (c u) r -> p c r u", u=2),
+                )
+
+        def quantise_x(j):
+            width = PAIR * C // PACK
+            x_codes[j] = stream.tile([P, width], U32, name="x_codes", tag="x_codes", align_bytes=64)
+            x_scales[j] = stream.tile(
+                [P, width], U8, name="x_scales", tag="x_scales", align_bytes=64
+            )
+            nc.vector.quantize_mx(
+                out=x_codes[j][:].bitcast(FP8X4), scales=x_scales[j][:], in_=x_grouped[j][:]
+            )
+
+        def project(j):
+            acc[j] = []
+            for t in range(PAIR):
+                bank = psum.tile([P, 2 * E], F32, name="acc", tag="acc", bufs=2 * PAIR)
+                for c in range(C_PASSES):
+                    cols = slice((t * C_PASSES + c) * P, (t * C_PASSES + c + 1) * P)
+                    nc.tensor.matmul_mx(
+                        out=bank[:],
+                        lhsT=x_codes[j][:, cols].bitcast(FP8X4),
+                        lhsT_scale=x_scales[j][:, cols],
+                        rhs=w_codes[:, c, :].bitcast(FP8X4),
+                        rhs_scale=w_scales[:, c, :],
+                        start=(c == 0),
+                        stop=(c == C_PASSES - 1),
+                    )
+                acc[j].append(bank)
+
+        def add_bias(j):
+            i, h = divmod(j, PAIRS_PER_GROUP)
+            if h == 0:
+                v_rows[i] = stream.tile([P, PACK, E], F32, name="v_rows", tag="v_rows", bufs=3)
+            kb[j] = stream.tile([P, PAIR, E], F32, name="kb", tag="kb")
+            k_sum[j] = small.tile([P, PAIR], F32, name="k_sum", tag="k_sum")
+            for t in range(PAIR):
+                nc.vector.scalar_tensor_tensor(
+                    out=kb[j][:, t, :],
+                    in0=acc[j][t][:, 0:E],
+                    scalar=1.0,
+                    in1=bias[:, 0:E],
+                    op0=ALU.mult,
+                    op1=ALU.add,
+                    accum_out=k_sum[j][:, t : t + 1],
+                )
+                nc.vector.tensor_tensor(
+                    out=v_rows[i][:, h * PAIR + t, :],
+                    in0=acc[j][t][:, E : 2 * E],
+                    in1=bias[:, E : 2 * E],
+                    op=ALU.add,
+                )
+
+        def negate_mean(j):
+            neg_mean[j] = small.tile([P, PAIR], F32, name="neg_mean", tag="neg_mean")
+            nc.gpsimd.tensor_scalar(
+                out=neg_mean[j][:], in0=k_sum[j][:], scalar1=-1.0 / E, scalar2=0.0,
+                op0=ALU.mult, op1=ALU.add,
+            )
+
+        def square_centred(j):
+            f[j] = stream.tile([P, PAIR, E], F32, name="f", tag="f")
+            f_sum[j] = small.tile([P, PAIR], F32, name="f_sum", tag="f_sum")
+            for t in range(PAIR):
+                nc.scalar.activation(
+                    out=f[j][:, t, :],
+                    in_=kb[j][:, t, :],
+                    func=ACT.Square,
+                    bias=neg_mean[j][:, t : t + 1],
+                    scale=1.0,
+                    accum_out=f_sum[j][:, t : t + 1],
+                )
+
+        def add_eps(j):
+            f_sum_eps[j] = small.tile([P, PAIR], F32, name="f_sum_eps", tag="f_sum_eps")
+            nc.gpsimd.tensor_scalar(
+                out=f_sum_eps[j][:], in0=f_sum[j][:], scalar1=EPS_SUM, scalar2=1.0,
+                op0=ALU.add, op1=ALU.mult,
+            )
+
+        def invert_sum(j):
+            r[j] = small.tile([P, PAIR], F32, name="r", tag="r")
+            nc.vector.reciprocal(out=r[j][:], in_=f_sum_eps[j][:])
+
+        def normalise(j):
+            i, h = divmod(j, PAIRS_PER_GROUP)
+            if h == 0:
+                g_rows[i] = stream.tile([P, PACK, E], F32, name="g_rows", tag="g_rows", bufs=6)
+            for t in range(PAIR):
+                nc.gpsimd.tensor_scalar(
+                    out=g_rows[i][:, h * PAIR + t, :], in0=f[j][:, t, :],
+                    scalar1=r[j][:, t : t + 1], scalar2=0.0, op0=ALU.mult, op1=ALU.add,
+                )
+
+        def transpose_g(j):
+            i, h = divmod(j, PAIRS_PER_GROUP)
+            g_t[j] = psum.tile([P, E_BLOCKS, PAIR, P], F32, name="g_t", tag="g_t")
+            for m in range(E_BLOCKS):
+                for t in range(PAIR):
+                    nc.tensor.transpose(
+                        g_t[j][:, m, t, :], g_rows[i][:, h * PAIR + t, m * P : (m + 1) * P], ident[:]
+                    )
+
+        def square_norm(j):
+            b, part = divmod(j, PAIRS_PER_BATCH)
+            if part == 0:
+                norm_parts[b] = small.tile(
+                    [P, E_BLOCKS, PAIRS_PER_BATCH], F32, name="norm_parts", tag="norm_parts", bufs=2
+                )
+            for m in range(E_BLOCKS):
+                nc.scalar.activation(
+                    out=squares[:],
+                    in_=g_t[j][:, m].rearrange("p t r -> p (t r)"),
+                    func=ACT.Square,
+                    accum_out=norm_parts[b][:, m, part : part + 1],
+                )
+
+        def store_v(i):
+            nc.sync.dma_start(out=v_groups[i], in_=v_rows[i][:])
+
+        def round_v(i):
+            v_grouped[i] = stream.tile(
+                [P, E, PACK], BF16, name="v_grouped", tag="v_grouped", align_bytes=64
+            )
+            nc.gpsimd.tensor_scalar(
+                out=v_grouped[i][:], in0=v_rows[i][:].rearrange("p t e -> p e t"),
+                scalar1=1.0, scalar2=0.0, op0=ALU.mult, op1=ALU.add,
+            )
+
+        def quantise_v(i):
+            b, s = divmod(i, GROUPS_PER_BATCH)
+            if s == 0:
+                v_codes[b] = stream.tile(
+                    [P, GROUPS_PER_BATCH, E], U32, name="v_codes", tag="v_codes", bufs=3,
+                    align_bytes=64,
+                )
+                v_scales[b] = stream.tile(
+                    [P, GROUPS_PER_BATCH, E], U8, name="v_scales", tag="v_scales", bufs=3,
+                    align_bytes=64,
+                )
+            nc.vector.quantize_mx(
+                out=v_codes[b][:, s, :].bitcast(FP8X4),
+                scales=v_scales[b][:, s, :],
+                in_=v_grouped[i][:].rearrange("p e t -> p (e t)"),
+            )
+
+        def sum_norm(b):
+            norm_sq[b] = small.tile([P, E_BLOCKS], F32, name="norm_sq", tag="norm_sq")
+            nc.vector.tensor_reduce(out=norm_sq[b][:], in_=norm_parts[b][:], axis=AXIS.X, op=ALU.add)
+            nc.vector.tensor_scalar_max(norm_sq[b][:], norm_sq[b][:], EPS_NORM * EPS_NORM)
+
+        def root_norm(b):
+            norm[b] = small.tile([P, E_BLOCKS], F32, name="norm", tag="norm")
+            nc.scalar.sqrt(norm[b][:], norm_sq[b][:])
+
+        def invert_norm(b):
+            r_norm[b] = small.tile([P, E_BLOCKS], F32, name="r_norm", tag="r_norm")
+            nc.vector.reciprocal(out=r_norm[b][:], in_=norm[b][:])
+
+        def spread_norm(b):
+            r_norm_ps[b] = psum.tile([P, E], F32, name="r_norm_ps", tag="batch")
+            for m in range(E_BLOCKS):
+                nc.tensor.matmul(
+                    out=r_norm_ps[b][:, m * P : (m + 1) * P],
+                    lhsT=r_norm[b][:, m : m + 1].to_broadcast([P, P]),
+                    rhs=ident[:],
+                    start=True,
+                    stop=True,
+                )
+
+        def copy_norm(b):
+            r_norm_rows[b] = stream.tile([P, E], F32, name="r_norm_rows", tag="r_norm_rows")
+            nc.scalar.copy(out=r_norm_rows[b][:], in_=r_norm_ps[b][:])
+
+        def scale_k2(b, s):
+            i = b * GROUPS_PER_BATCH + s
+            k2_grouped[i] = stream.tile(
+                [P, E, PACK], BF16, name="k2_grouped", tag="k2_grouped", align_bytes=64
+            )
+            nc.vector.tensor_tensor(
+                out=k2_grouped[i][:],
+                in0=g_rows[i][:].rearrange("p t e -> p e t"),
+                in1=r_norm_rows[b][:].unsqueeze(2).to_broadcast([P, E, PACK]),
+                op=ALU.mult,
+            )
+
+        def quantise_k2(b, s):
+            i = b * GROUPS_PER_BATCH + s
+            if s == 0:
+                k2_codes[b] = stream.tile(
+                    [P, GROUPS_PER_BATCH, E], U32, name="k2_codes", tag="k2_codes", align_bytes=64
+                )
+                k2_scales[b] = stream.tile(
+                    [P, GROUPS_PER_BATCH, E], U8, name="k2_scales", tag="k2_scales", align_bytes=64
+                )
+            nc.vector.quantize_mx(
+                out=k2_codes[b][:, s, :].bitcast(FP8X4),
+                scales=k2_scales[b][:, s, :],
+                in_=k2_grouped[i][:].rearrange("p e t -> p (e t)"),
+            )
+
+        def multiply_kv(b):
+            kv_ps[b] = psum.tile([P, E_BLOCKS, E], F32, name="kv_ps", tag="batch")
+            for m in range(E_BLOCKS):
+                for s in range(GROUPS_PER_BATCH):
+                    nc.tensor.matmul_mx(
+                        out=kv_ps[b][:, m, :],
+                        lhsT=k2_codes[b][:, s, m * P : (m + 1) * P].bitcast(FP8X4),
+                        lhsT_scale=k2_scales[b][:, s, m * P : (m + 1) * P],
+                        rhs=v_codes[b][:, s, :].bitcast(FP8X4),
+                        rhs_scale=v_scales[b][:, s, :],
+                        start=(s == 0),
+                        stop=(s == GROUPS_PER_BATCH - 1),
+                    )
+
+        def store_kv(b):
+            kv_rows = stream.tile([P, E_BLOCKS, E], F32, name="kv_rows", tag="kv_rows")
+            nc.scalar.copy(out=kv_rows[:], in_=kv_ps[b][:])
+            nc.sync.dma_start(out=out_0[b].rearrange("(m p) e -> p m e", p=P), in_=kv_rows[:])
+
+        for s in range(-1, LAST_STEP + 1):
+            b, phase = divmod(s - NORM_STEP, PAIRS_PER_BATCH)
+            batch_ok = 0 <= b < B
+
+            if in_range(s):
+                quantise_x(s)
+            if in_range(s + 1):
+                transpose_x(s + 1)
+                load_x(s + 1 + X_BUFS)
+            if in_range(s - 4):
+                transpose_g(s - 4)
+            if batch_ok and phase == 1:
+                spread_norm(b)
+            if in_range(s):
+                project(s)
+            if batch_ok and phase == 7:
+                multiply_kv(b)
+
+            if in_range(s - 3):
+                normalise(s - 3)
+            if in_range(s - 2):
+                square_centred(s - 2)
+                add_eps(s - 2)
+            if batch_ok and phase == 0:
+                sum_norm(b)
+                root_norm(b)
+            if in_range(s + 1):
+                regroup_x(s + 1)
+            if in_range(s - 4):
+                square_norm(s - 4)
+            if batch_ok and phase == 1:
+                copy_norm(b)
+            if 0 <= b - 1 and phase == 0:
+                store_kv(b - 1)
+
+            if in_range(s - 1):
+                add_bias(s - 1)
+                negate_mean(s - 1)
+                if (s - 1) % PAIRS_PER_GROUP == PAIRS_PER_GROUP - 1:
+                    store_v((s - 1) // PAIRS_PER_GROUP)
+                    round_v((s - 1) // PAIRS_PER_GROUP)
+            if in_range(s - 2):
+                invert_sum(s - 2)
+                if (s - 2) % PAIRS_PER_GROUP == PAIRS_PER_GROUP - 1:
+                    quantise_v((s - 2) // PAIRS_PER_GROUP)
+            if batch_ok and phase == 0:
+                invert_norm(b)
+            if batch_ok and 3 <= phase < 3 + GROUPS_PER_BATCH:
+                quantise_k2(b, phase - 3)
+            if batch_ok and 2 <= phase < 2 + GROUPS_PER_BATCH:
+                scale_k2(b, phase - 2)

@@ -102,7 +102,7 @@ def tile_essattn_pa_t_kernel(tc, x, wk, bk, wv, bv, out_0, out_1):
         bias = const.tile([P, 2 * E], F32)
         nc.vector.tensor_copy(out=bias[:], in_=bias_bf[:])
 
-        squares = const.tile([P, PAIR * P], BF16)
+        squares = const.tile([P, PACK * P], BF16)
 
         def in_range(j):
             return 0 <= j < PAIRS
@@ -214,35 +214,29 @@ def tile_essattn_pa_t_kernel(tc, x, wk, bk, wv, bv, out_0, out_1):
         def normalise(j):
             i, h = divmod(j, PAIRS_PER_GROUP)
             if h == 0:
-                g_rows[i] = stream.tile([P, PACK, E], F32, name="g_rows", tag="g_rows", bufs=6)
+                g_rows[i] = stream.tile([P, PACK, E], F32, name="g_rows", tag="g_rows", bufs=7)
             for t in range(PAIR):
-                nc.gpsimd.tensor_scalar(
-                    out=g_rows[i][:, h * PAIR + t, :], in0=f[j][:, t, :],
-                    scalar1=r[j][:, t : t + 1], scalar2=0.0, op0=ALU.mult, op1=ALU.add,
+                nc.vector.tensor_scalar_mul(
+                    out=g_rows[i][:, h * PAIR + t, :], in0=f[j][:, t, :], scalar1=r[j][:, t : t + 1]
                 )
 
-        def transpose_g(j):
-            i, h = divmod(j, PAIRS_PER_GROUP)
-            g_t[j] = psum.tile([P, E_BLOCKS, PAIR, P], F32, name="g_t", tag="g_t")
-            for m in range(E_BLOCKS):
-                for t in range(PAIR):
-                    nc.tensor.transpose(
-                        g_t[j][:, m, t, :], g_rows[i][:, h * PAIR + t, m * P : (m + 1) * P], ident[:]
-                    )
+        def transpose_g(i, m):
+            g_t[i, m] = psum.tile([P, PACK, P], F32, name="g_t", tag="g_t")
+            for t in range(PACK):
+                nc.tensor.transpose(g_t[i, m][:, t, :], g_rows[i][:, t, m * P : (m + 1) * P], ident[:])
 
-        def square_norm(j):
-            b, part = divmod(j, PAIRS_PER_BATCH)
-            if part == 0:
+        def square_norm(i, m):
+            b, s = divmod(i, GROUPS_PER_BATCH)
+            if s == 0 and m == 0:
                 norm_parts[b] = small.tile(
-                    [P, E_BLOCKS, PAIRS_PER_BATCH], F32, name="norm_parts", tag="norm_parts", bufs=2
+                    [P, E_BLOCKS, GROUPS_PER_BATCH], F32, name="norm_parts", tag="norm_parts", bufs=2
                 )
-            for m in range(E_BLOCKS):
-                nc.scalar.activation(
-                    out=squares[:],
-                    in_=g_t[j][:, m].rearrange("p t r -> p (t r)"),
-                    func=ACT.Square,
-                    accum_out=norm_parts[b][:, m, part : part + 1],
-                )
+            nc.scalar.activation(
+                out=squares[:],
+                in_=g_t[i, m][:].rearrange("p t r -> p (t r)"),
+                func=ACT.Square,
+                accum_out=norm_parts[b][:, m, s : s + 1],
+            )
 
         def store_v(i):
             nc.sync.dma_start(out=v_groups[i], in_=v_rows[i][:])
@@ -251,10 +245,7 @@ def tile_essattn_pa_t_kernel(tc, x, wk, bk, wv, bv, out_0, out_1):
             v_grouped[i] = stream.tile(
                 [P, E, PACK], BF16, name="v_grouped", tag="v_grouped", align_bytes=64
             )
-            nc.gpsimd.tensor_scalar(
-                out=v_grouped[i][:], in0=v_rows[i][:].rearrange("p t e -> p e t"),
-                scalar1=1.0, scalar2=0.0, op0=ALU.mult, op1=ALU.add,
-            )
+            nc.scalar.copy(out=v_grouped[i][:], in_=v_rows[i][:].rearrange("p t e -> p e t"))
 
         def quantise_v(i):
             b, s = divmod(i, GROUPS_PER_BATCH)
@@ -347,17 +338,22 @@ def tile_essattn_pa_t_kernel(tc, x, wk, bk, wv, bv, out_0, out_1):
             nc.scalar.copy(out=kv_rows[:], in_=kv_ps[b][:])
             nc.sync.dma_start(out=out_0[b].rearrange("(m p) e -> p m e", p=P), in_=kv_rows[:])
 
+        def second_of_group(j):
+            return in_range(j) and j % PAIRS_PER_GROUP == PAIRS_PER_GROUP - 1
+
         for s in range(-1, LAST_STEP + 1):
             b, phase = divmod(s - NORM_STEP, PAIRS_PER_BATCH)
             batch_ok = 0 <= b < B
+            g_group, g_block = divmod(s - 4, E_BLOCKS)
+            g_ok = 0 <= g_group < B * GROUPS_PER_BATCH
 
             if in_range(s):
                 quantise_x(s)
             if in_range(s + 1):
                 transpose_x(s + 1)
                 load_x(s + 1 + X_BUFS)
-            if in_range(s - 4):
-                transpose_g(s - 4)
+            if g_ok:
+                transpose_g(g_group, g_block)
             if batch_ok and phase == 1:
                 spread_norm(b)
             if in_range(s):
@@ -365,8 +361,6 @@ def tile_essattn_pa_t_kernel(tc, x, wk, bk, wv, bv, out_0, out_1):
             if batch_ok and phase == 7:
                 multiply_kv(b)
 
-            if in_range(s - 3):
-                normalise(s - 3)
             if in_range(s - 2):
                 square_centred(s - 2)
                 add_eps(s - 2)
@@ -375,8 +369,10 @@ def tile_essattn_pa_t_kernel(tc, x, wk, bk, wv, bv, out_0, out_1):
                 root_norm(b)
             if in_range(s + 1):
                 regroup_x(s + 1)
-            if in_range(s - 4):
-                square_norm(s - 4)
+            if g_ok:
+                square_norm(g_group, g_block)
+            if second_of_group(s - 2):
+                round_v((s - 2) // PAIRS_PER_GROUP)
             if batch_ok and phase == 1:
                 copy_norm(b)
             if 0 <= b - 1 and phase == 0:
@@ -385,16 +381,17 @@ def tile_essattn_pa_t_kernel(tc, x, wk, bk, wv, bv, out_0, out_1):
             if in_range(s - 1):
                 add_bias(s - 1)
                 negate_mean(s - 1)
-                if (s - 1) % PAIRS_PER_GROUP == PAIRS_PER_GROUP - 1:
-                    store_v((s - 1) // PAIRS_PER_GROUP)
-                    round_v((s - 1) // PAIRS_PER_GROUP)
+            if second_of_group(s - 1):
+                store_v((s - 1) // PAIRS_PER_GROUP)
             if in_range(s - 2):
                 invert_sum(s - 2)
-                if (s - 2) % PAIRS_PER_GROUP == PAIRS_PER_GROUP - 1:
-                    quantise_v((s - 2) // PAIRS_PER_GROUP)
             if batch_ok and phase == 0:
                 invert_norm(b)
+            if second_of_group(s - 3):
+                quantise_v((s - 3) // PAIRS_PER_GROUP)
             if batch_ok and 3 <= phase < 3 + GROUPS_PER_BATCH:
                 quantise_k2(b, phase - 3)
+            if in_range(s - 2):
+                normalise(s - 2)
             if batch_ok and 2 <= phase < 2 + GROUPS_PER_BATCH:
                 scale_k2(b, phase - 2)

@@ -107,15 +107,12 @@ def tile_essattn_pa_t_kernel(tc, x, wk, bk, wv, bv, out_0, out_1):
         def in_range(j):
             return 0 <= j < PAIRS
 
-        def transpose_x(j):
+        def transpose_x(j, t):
             words = x_rows[j][:].bitcast(F32)
-            x_t[j] = []
-            for t in range(PAIR):
-                bank = psum.tile([P, WORDS // P, P], F32, name="x_t", tag="x_t", bufs=PAIR)
-                for q in range(WORDS // P):
-                    first = t * WORDS + q * P
-                    nc.tensor.transpose(bank[:, q, :], words[:, first : first + P], ident[:])
-                x_t[j].append(bank)
+            x_t[j, t] = psum.tile([P, WORDS // P, P], F32, name="x_t", tag="x_t", bufs=PAIR)
+            for q in range(WORDS // P):
+                first = t * WORDS + q * P
+                nc.tensor.transpose(x_t[j, t][:, q, :], words[:, first : first + P], ident[:])
 
         def regroup_x(j):
             x_grouped[j] = stream.tile(
@@ -127,7 +124,7 @@ def tile_essattn_pa_t_kernel(tc, x, wk, bk, wv, bv, out_0, out_1):
                     out=words[:, t * WORDS : (t + 1) * WORDS].rearrange(
                         "p (c r u) -> p c r u", c=C_PASSES, u=2
                     ),
-                    in_=x_t[j][t][:].rearrange("p (c u) r -> p c r u", u=2),
+                    in_=x_t[j, t][:].rearrange("p (c u) r -> p c r u", u=2),
                 )
 
         def quantise_x(j):
@@ -140,22 +137,19 @@ def tile_essattn_pa_t_kernel(tc, x, wk, bk, wv, bv, out_0, out_1):
                 out=x_codes[j][:].bitcast(FP8X4), scales=x_scales[j][:], in_=x_grouped[j][:]
             )
 
-        def project(j):
-            acc[j] = []
-            for t in range(PAIR):
-                bank = psum.tile([P, 2 * E], F32, name="acc", tag="acc", bufs=2 * PAIR)
-                for c in range(C_PASSES):
-                    cols = slice((t * C_PASSES + c) * P, (t * C_PASSES + c + 1) * P)
-                    nc.tensor.matmul_mx(
-                        out=bank[:],
-                        lhsT=x_codes[j][:, cols].bitcast(FP8X4),
-                        lhsT_scale=x_scales[j][:, cols],
-                        rhs=w_codes[:, c, :].bitcast(FP8X4),
-                        rhs_scale=w_scales[:, c, :],
-                        start=(c == 0),
-                        stop=(c == C_PASSES - 1),
-                    )
-                acc[j].append(bank)
+        def project(j, t):
+            acc[j, t] = psum.tile([P, 2 * E], F32, name="acc", tag="acc", bufs=2 * PAIR)
+            for c in range(C_PASSES):
+                cols = slice((t * C_PASSES + c) * P, (t * C_PASSES + c + 1) * P)
+                nc.tensor.matmul_mx(
+                    out=acc[j, t][:],
+                    lhsT=x_codes[j][:, cols].bitcast(FP8X4),
+                    lhsT_scale=x_scales[j][:, cols],
+                    rhs=w_codes[:, c, :].bitcast(FP8X4),
+                    rhs_scale=w_scales[:, c, :],
+                    start=(c == 0),
+                    stop=(c == C_PASSES - 1),
+                )
 
         def add_bias(j):
             i, h = divmod(j, PAIRS_PER_GROUP)
@@ -166,7 +160,7 @@ def tile_essattn_pa_t_kernel(tc, x, wk, bk, wv, bv, out_0, out_1):
             for t in range(PAIR):
                 nc.vector.scalar_tensor_tensor(
                     out=kb[j][:, t, :],
-                    in0=acc[j][t][:, 0:E],
+                    in0=acc[j, t][:, 0:E],
                     scalar=1.0,
                     in1=bias[:, 0:E],
                     op0=ALU.mult,
@@ -175,7 +169,7 @@ def tile_essattn_pa_t_kernel(tc, x, wk, bk, wv, bv, out_0, out_1):
                 )
                 nc.vector.tensor_tensor(
                     out=v_rows[i][:, h * PAIR + t, :],
-                    in0=acc[j][t][:, E : 2 * E],
+                    in0=acc[j, t][:, E : 2 * E],
                     in1=bias[:, E : 2 * E],
                     op=ALU.add,
                 )
@@ -220,14 +214,15 @@ def tile_essattn_pa_t_kernel(tc, x, wk, bk, wv, bv, out_0, out_1):
                     out=g_rows[i][:, h * PAIR + t, :], in0=f[j][:, t, :], scalar1=r[j][:, t : t + 1]
                 )
 
-        def transpose_g(i, m):
-            g_t[i, m] = psum.tile([P, PACK, P], F32, name="g_t", tag="g_t")
-            for t in range(PACK):
+        def transpose_g(i, m, h):
+            if h == 0:
+                g_t[i, m] = psum.tile([P, PACK, P], F32, name="g_t", tag="g_t")
+            for t in range(h * PAIR, (h + 1) * PAIR):
                 nc.tensor.transpose(g_t[i, m][:, t, :], g_rows[i][:, t, m * P : (m + 1) * P], ident[:])
 
         def square_norm(i, m):
-            b, s = divmod(i, GROUPS_PER_BATCH)
-            if s == 0 and m == 0:
+            b, grp = divmod(i, GROUPS_PER_BATCH)
+            if grp == 0 and m == 0:
                 norm_parts[b] = small.tile(
                     [P, E_BLOCKS, GROUPS_PER_BATCH], F32, name="norm_parts", tag="norm_parts", bufs=2
                 )
@@ -235,7 +230,7 @@ def tile_essattn_pa_t_kernel(tc, x, wk, bk, wv, bv, out_0, out_1):
                 out=squares[:],
                 in_=g_t[i, m][:].rearrange("p t r -> p (t r)"),
                 func=ACT.Square,
-                accum_out=norm_parts[b][:, m, s : s + 1],
+                accum_out=norm_parts[b][:, m, grp : grp + 1],
             )
 
         def store_v(i):
@@ -248,8 +243,8 @@ def tile_essattn_pa_t_kernel(tc, x, wk, bk, wv, bv, out_0, out_1):
             nc.scalar.copy(out=v_grouped[i][:], in_=v_rows[i][:].rearrange("p t e -> p e t"))
 
         def quantise_v(i):
-            b, s = divmod(i, GROUPS_PER_BATCH)
-            if s == 0:
+            b, grp = divmod(i, GROUPS_PER_BATCH)
+            if grp == 0:
                 v_codes[b] = stream.tile(
                     [P, GROUPS_PER_BATCH, E], U32, name="v_codes", tag="v_codes", bufs=3,
                     align_bytes=64,
@@ -259,8 +254,8 @@ def tile_essattn_pa_t_kernel(tc, x, wk, bk, wv, bv, out_0, out_1):
                     align_bytes=64,
                 )
             nc.vector.quantize_mx(
-                out=v_codes[b][:, s, :].bitcast(FP8X4),
-                scales=v_scales[b][:, s, :],
+                out=v_codes[b][:, grp, :].bitcast(FP8X4),
+                scales=v_scales[b][:, grp, :],
                 in_=v_grouped[i][:].rearrange("p e t -> p (e t)"),
             )
 
@@ -292,8 +287,8 @@ def tile_essattn_pa_t_kernel(tc, x, wk, bk, wv, bv, out_0, out_1):
             r_norm_rows[b] = stream.tile([P, E], F32, name="r_norm_rows", tag="r_norm_rows")
             nc.scalar.copy(out=r_norm_rows[b][:], in_=r_norm_ps[b][:])
 
-        def scale_k2(b, s):
-            i = b * GROUPS_PER_BATCH + s
+        def scale_k2(b, grp):
+            i = b * GROUPS_PER_BATCH + grp
             k2_grouped[i] = stream.tile(
                 [P, E, PACK], BF16, name="k2_grouped", tag="k2_grouped", align_bytes=64
             )
@@ -304,9 +299,9 @@ def tile_essattn_pa_t_kernel(tc, x, wk, bk, wv, bv, out_0, out_1):
                 op=ALU.mult,
             )
 
-        def quantise_k2(b, s):
-            i = b * GROUPS_PER_BATCH + s
-            if s == 0:
+        def quantise_k2(b, grp):
+            i = b * GROUPS_PER_BATCH + grp
+            if grp == 0:
                 k2_codes[b] = stream.tile(
                     [P, GROUPS_PER_BATCH, E], U32, name="k2_codes", tag="k2_codes", align_bytes=64
                 )
@@ -314,23 +309,23 @@ def tile_essattn_pa_t_kernel(tc, x, wk, bk, wv, bv, out_0, out_1):
                     [P, GROUPS_PER_BATCH, E], U8, name="k2_scales", tag="k2_scales", align_bytes=64
                 )
             nc.vector.quantize_mx(
-                out=k2_codes[b][:, s, :].bitcast(FP8X4),
-                scales=k2_scales[b][:, s, :],
+                out=k2_codes[b][:, grp, :].bitcast(FP8X4),
+                scales=k2_scales[b][:, grp, :],
                 in_=k2_grouped[i][:].rearrange("p e t -> p (e t)"),
             )
 
         def multiply_kv(b):
             kv_ps[b] = psum.tile([P, E_BLOCKS, E], F32, name="kv_ps", tag="batch")
             for m in range(E_BLOCKS):
-                for s in range(GROUPS_PER_BATCH):
+                for grp in range(GROUPS_PER_BATCH):
                     nc.tensor.matmul_mx(
                         out=kv_ps[b][:, m, :],
-                        lhsT=k2_codes[b][:, s, m * P : (m + 1) * P].bitcast(FP8X4),
-                        lhsT_scale=k2_scales[b][:, s, m * P : (m + 1) * P],
-                        rhs=v_codes[b][:, s, :].bitcast(FP8X4),
-                        rhs_scale=v_scales[b][:, s, :],
-                        start=(s == 0),
-                        stop=(s == GROUPS_PER_BATCH - 1),
+                        lhsT=k2_codes[b][:, grp, m * P : (m + 1) * P].bitcast(FP8X4),
+                        lhsT_scale=k2_scales[b][:, grp, m * P : (m + 1) * P],
+                        rhs=v_codes[b][:, grp, :].bitcast(FP8X4),
+                        rhs_scale=v_scales[b][:, grp, :],
+                        start=(grp == 0),
+                        stop=(grp == GROUPS_PER_BATCH - 1),
                     )
 
         def store_kv(b):
@@ -349,15 +344,16 @@ def tile_essattn_pa_t_kernel(tc, x, wk, bk, wv, bv, out_0, out_1):
 
             if in_range(s):
                 quantise_x(s)
-            if in_range(s + 1):
-                transpose_x(s + 1)
-                load_x(s + 1 + X_BUFS)
-            if g_ok:
-                transpose_g(g_group, g_block)
             if batch_ok and phase == 1:
                 spread_norm(b)
-            if in_range(s):
-                project(s)
+            for t in range(PAIR):
+                if in_range(s + 1):
+                    transpose_x(s + 1, t)
+                if g_ok:
+                    transpose_g(g_group, g_block, t)
+                if in_range(s):
+                    project(s, t)
+            load_x(s + 1 + X_BUFS)
             if batch_ok and phase == 7:
                 multiply_kv(b)
 

@@ -30,7 +30,9 @@ PAIRS = B * PAIRS_PER_BATCH
 E_BLOCKS = E // P
 
 X_BUFS = 6
-NORM_STEP = PAIRS_PER_BATCH + 4
+V_LAG = PAIRS_PER_BATCH
+NORM_STEP = PAIRS_PER_BATCH + 5
+G_LAG = 5
 LAST_STEP = NORM_STEP + B * PAIRS_PER_BATCH
 
 
@@ -46,7 +48,7 @@ def tile_essattn_pa_t_kernel(tc, x, wk, bk, wv, bv, out_0, out_1):
         small = ctx.enter_context(tc.tile_pool(name="small", bufs=4))
         psum = ctx.enter_context(tc.psum_pool(name="psum", bufs=1))
 
-        x_rows, x_t, x_grouped, x_codes, x_scales, acc = {}, {}, {}, {}, {}, {}
+        x_rows, x_t, x_grouped, x_codes, x_scales, k_acc, v_acc = {}, {}, {}, {}, {}, {}, {}
         kb, k_sum, neg_mean, f, f_sum, f_sum_eps, r = {}, {}, {}, {}, {}, {}, {}
         g_rows, g_t, v_rows, v_grouped = {}, {}, {}, {}
         norm_parts, norm_sq, norm, r_norm, r_norm_ps, r_norm_rows = {}, {}, {}, {}, {}, {}
@@ -107,12 +109,15 @@ def tile_essattn_pa_t_kernel(tc, x, wk, bk, wv, bv, out_0, out_1):
         def in_range(j):
             return 0 <= j < PAIRS
 
-        def transpose_x(j, t):
+        def transpose_x(j):
             words = x_rows[j][:].bitcast(F32)
-            x_t[j, t] = psum.tile([P, WORDS // P, P], F32, name="x_t", tag="x_t", bufs=PAIR)
-            for q in range(WORDS // P):
-                first = t * WORDS + q * P
-                nc.tensor.transpose(x_t[j, t][:, q, :], words[:, first : first + P], ident[:])
+            x_t[j] = []
+            for t in range(PAIR):
+                bank = psum.tile([P, WORDS // P, P], F32, name="x_t", tag="x_t", bufs=PAIR)
+                for q in range(WORDS // P):
+                    first = t * WORDS + q * P
+                    nc.tensor.transpose(bank[:, q, :], words[:, first : first + P], ident[:])
+                x_t[j].append(bank)
 
         def regroup_x(j):
             x_grouped[j] = stream.tile(
@@ -124,55 +129,67 @@ def tile_essattn_pa_t_kernel(tc, x, wk, bk, wv, bv, out_0, out_1):
                     out=words[:, t * WORDS : (t + 1) * WORDS].rearrange(
                         "p (c r u) -> p c r u", c=C_PASSES, u=2
                     ),
-                    in_=x_t[j, t][:].rearrange("p (c u) r -> p c r u", u=2),
+                    in_=x_t[j][t][:].rearrange("p (c u) r -> p c r u", u=2),
                 )
 
         def quantise_x(j):
             width = PAIR * C // PACK
-            x_codes[j] = stream.tile([P, width], U32, name="x_codes", tag="x_codes", align_bytes=64)
+            x_codes[j] = stream.tile(
+                [P, width], U32, name="x_codes", tag="x_codes", bufs=V_LAG + 2, align_bytes=64
+            )
             x_scales[j] = stream.tile(
-                [P, width], U8, name="x_scales", tag="x_scales", align_bytes=64
+                [P, width], U8, name="x_scales", tag="x_scales", bufs=V_LAG + 2, align_bytes=64
             )
             nc.vector.quantize_mx(
                 out=x_codes[j][:].bitcast(FP8X4), scales=x_scales[j][:], in_=x_grouped[j][:]
             )
 
-        def project(j, t):
-            acc[j, t] = psum.tile([P, 2 * E], F32, name="acc", tag="acc", bufs=2 * PAIR)
-            for c in range(C_PASSES):
-                cols = slice((t * C_PASSES + c) * P, (t * C_PASSES + c + 1) * P)
-                nc.tensor.matmul_mx(
-                    out=acc[j, t][:],
-                    lhsT=x_codes[j][:, cols].bitcast(FP8X4),
-                    lhsT_scale=x_scales[j][:, cols],
-                    rhs=w_codes[:, c, :].bitcast(FP8X4),
-                    rhs_scale=w_scales[:, c, :],
-                    start=(c == 0),
-                    stop=(c == C_PASSES - 1),
-                )
+        def project(j, side, bank):
+            for t in range(PAIR):
+                for c in range(C_PASSES):
+                    cols = slice((t * C_PASSES + c) * P, (t * C_PASSES + c + 1) * P)
+                    nc.tensor.matmul_mx(
+                        out=bank[:, t, :],
+                        lhsT=x_codes[j][:, cols].bitcast(FP8X4),
+                        lhsT_scale=x_scales[j][:, cols],
+                        rhs=w_codes[:, c, side * E : (side + 1) * E].bitcast(FP8X4),
+                        rhs_scale=w_scales[:, c, side * E : (side + 1) * E],
+                        start=(c == 0),
+                        stop=(c == C_PASSES - 1),
+                    )
 
-        def add_bias(j):
-            i, h = divmod(j, PAIRS_PER_GROUP)
-            if h == 0:
-                v_rows[i] = stream.tile([P, PACK, E], F32, name="v_rows", tag="v_rows", bufs=3)
+        def project_k(j):
+            k_acc[j] = psum.tile([P, PAIR, E], F32, name="k_acc", tag="k_acc", bufs=2)
+            project(j, 0, k_acc[j])
+
+        def project_v(j):
+            v_acc[j] = psum.tile([P, PAIR, E], F32, name="v_acc", tag="v_acc", bufs=2)
+            project(j, 1, v_acc[j])
+
+        def add_bias_k(j):
             kb[j] = stream.tile([P, PAIR, E], F32, name="kb", tag="kb")
             k_sum[j] = small.tile([P, PAIR], F32, name="k_sum", tag="k_sum")
             for t in range(PAIR):
                 nc.vector.scalar_tensor_tensor(
                     out=kb[j][:, t, :],
-                    in0=acc[j, t][:, 0:E],
+                    in0=k_acc[j][:, t, :],
                     scalar=1.0,
                     in1=bias[:, 0:E],
                     op0=ALU.mult,
                     op1=ALU.add,
                     accum_out=k_sum[j][:, t : t + 1],
                 )
-                nc.vector.tensor_tensor(
-                    out=v_rows[i][:, h * PAIR + t, :],
-                    in0=acc[j, t][:, E : 2 * E],
-                    in1=bias[:, E : 2 * E],
-                    op=ALU.add,
-                )
+
+        def add_bias_v(j):
+            i, h = divmod(j, PAIRS_PER_GROUP)
+            if h == 0:
+                v_rows[i] = stream.tile([P, PACK, E], F32, name="v_rows", tag="v_rows", bufs=3)
+            nc.vector.tensor_tensor(
+                out=v_rows[i][:, h * PAIR : (h + 1) * PAIR, :],
+                in0=v_acc[j][:],
+                in1=bias[:, E : 2 * E].unsqueeze(1).to_broadcast([P, PAIR, E]),
+                op=ALU.add,
+            )
 
         def negate_mean(j):
             neg_mean[j] = small.tile([P, PAIR], F32, name="neg_mean", tag="neg_mean")
@@ -182,7 +199,7 @@ def tile_essattn_pa_t_kernel(tc, x, wk, bk, wv, bv, out_0, out_1):
             )
 
         def square_centred(j):
-            f[j] = stream.tile([P, PAIR, E], F32, name="f", tag="f")
+            f[j] = stream.tile([P, PAIR, E], F32, name="f", tag="f", bufs=3)
             f_sum[j] = small.tile([P, PAIR], F32, name="f_sum", tag="f_sum")
             for t in range(PAIR):
                 nc.scalar.activation(
@@ -205,19 +222,24 @@ def tile_essattn_pa_t_kernel(tc, x, wk, bk, wv, bv, out_0, out_1):
             r[j] = small.tile([P, PAIR], F32, name="r", tag="r")
             nc.vector.reciprocal(out=r[j][:], in_=f_sum_eps[j][:])
 
-        def normalise(j):
+        def normalise_first(j):
             i, h = divmod(j, PAIRS_PER_GROUP)
             if h == 0:
                 g_rows[i] = stream.tile([P, PACK, E], F32, name="g_rows", tag="g_rows", bufs=7)
-            for t in range(PAIR):
-                nc.vector.tensor_scalar_mul(
-                    out=g_rows[i][:, h * PAIR + t, :], in0=f[j][:, t, :], scalar1=r[j][:, t : t + 1]
-                )
+            nc.vector.tensor_scalar_mul(
+                out=g_rows[i][:, h * PAIR, :], in0=f[j][:, 0, :], scalar1=r[j][:, 0:1]
+            )
 
-        def transpose_g(i, m, h):
-            if h == 0:
-                g_t[i, m] = psum.tile([P, PACK, P], F32, name="g_t", tag="g_t")
-            for t in range(h * PAIR, (h + 1) * PAIR):
+        def normalise_second(j):
+            i, h = divmod(j, PAIRS_PER_GROUP)
+            nc.scalar.activation(
+                out=g_rows[i][:, h * PAIR + 1, :], in_=f[j][:, 1, :], func=ACT.Copy,
+                scale=r[j][:, 1:2],
+            )
+
+        def transpose_g(i, m):
+            g_t[i, m] = psum.tile([P, PACK, P], F32, name="g_t", tag="g_t")
+            for t in range(PACK):
                 nc.tensor.transpose(g_t[i, m][:, t, :], g_rows[i][:, t, m * P : (m + 1) * P], ident[:])
 
         def square_norm(i, m):
@@ -240,17 +262,17 @@ def tile_essattn_pa_t_kernel(tc, x, wk, bk, wv, bv, out_0, out_1):
             v_grouped[i] = stream.tile(
                 [P, E, PACK], BF16, name="v_grouped", tag="v_grouped", align_bytes=64
             )
-            nc.scalar.copy(out=v_grouped[i][:], in_=v_rows[i][:].rearrange("p t e -> p e t"))
+            nc.vector.tensor_copy(out=v_grouped[i][:], in_=v_rows[i][:].rearrange("p t e -> p e t"))
 
         def quantise_v(i):
             b, grp = divmod(i, GROUPS_PER_BATCH)
             if grp == 0:
                 v_codes[b] = stream.tile(
-                    [P, GROUPS_PER_BATCH, E], U32, name="v_codes", tag="v_codes", bufs=3,
+                    [P, GROUPS_PER_BATCH, E], U32, name="v_codes", tag="v_codes",
                     align_bytes=64,
                 )
                 v_scales[b] = stream.tile(
-                    [P, GROUPS_PER_BATCH, E], U8, name="v_scales", tag="v_scales", bufs=3,
+                    [P, GROUPS_PER_BATCH, E], U8, name="v_scales", tag="v_scales",
                     align_bytes=64,
                 )
             nc.vector.quantize_mx(
@@ -339,21 +361,22 @@ def tile_essattn_pa_t_kernel(tc, x, wk, bk, wv, bv, out_0, out_1):
         for s in range(-1, LAST_STEP + 1):
             b, phase = divmod(s - NORM_STEP, PAIRS_PER_BATCH)
             batch_ok = 0 <= b < B
-            g_group, g_block = divmod(s - 4, E_BLOCKS)
+            g_group, g_block = divmod(s - G_LAG, E_BLOCKS)
             g_ok = 0 <= g_group < B * GROUPS_PER_BATCH
 
             if in_range(s):
                 quantise_x(s)
+            if in_range(s + 1):
+                transpose_x(s + 1)
+            load_x(s + 1 + X_BUFS)
+            if g_ok:
+                transpose_g(g_group, g_block)
             if batch_ok and phase == 1:
                 spread_norm(b)
-            for t in range(PAIR):
-                if in_range(s + 1):
-                    transpose_x(s + 1, t)
-                if g_ok:
-                    transpose_g(g_group, g_block, t)
-                if in_range(s):
-                    project(s, t)
-            load_x(s + 1 + X_BUFS)
+            if in_range(s):
+                project_k(s)
+            if in_range(s - V_LAG):
+                project_v(s - V_LAG)
             if batch_ok and phase == 7:
                 multiply_kv(b)
 
@@ -365,29 +388,33 @@ def tile_essattn_pa_t_kernel(tc, x, wk, bk, wv, bv, out_0, out_1):
                 root_norm(b)
             if in_range(s + 1):
                 regroup_x(s + 1)
+            if in_range(s - 3):
+                normalise_second(s - 3)
             if g_ok:
                 square_norm(g_group, g_block)
-            if second_of_group(s - 2):
-                round_v((s - 2) // PAIRS_PER_GROUP)
             if batch_ok and phase == 1:
                 copy_norm(b)
             if 0 <= b - 1 and phase == 0:
                 store_kv(b - 1)
 
             if in_range(s - 1):
-                add_bias(s - 1)
+                add_bias_k(s - 1)
                 negate_mean(s - 1)
-            if second_of_group(s - 1):
-                store_v((s - 1) // PAIRS_PER_GROUP)
+            if in_range(s - V_LAG - 1):
+                add_bias_v(s - V_LAG - 1)
+            if second_of_group(s - V_LAG - 1):
+                store_v((s - V_LAG - 1) // PAIRS_PER_GROUP)
             if in_range(s - 2):
                 invert_sum(s - 2)
             if batch_ok and phase == 0:
                 invert_norm(b)
-            if second_of_group(s - 3):
-                quantise_v((s - 3) // PAIRS_PER_GROUP)
+            if second_of_group(s - V_LAG - 2):
+                quantise_v((s - V_LAG - 2) // PAIRS_PER_GROUP)
             if batch_ok and 3 <= phase < 3 + GROUPS_PER_BATCH:
                 quantise_k2(b, phase - 3)
             if in_range(s - 2):
-                normalise(s - 2)
+                normalise_first(s - 2)
+            if second_of_group(s - V_LAG - 1):
+                round_v((s - V_LAG - 1) // PAIRS_PER_GROUP)
             if batch_ok and 2 <= phase < 2 + GROUPS_PER_BATCH:
                 scale_k2(b, phase - 2)

@@ -10,7 +10,6 @@ U8 = mybir.dt.uint8
 FP8X4 = mybir.dt.float8_e4m3fn_x4
 ALU = mybir.AluOpType
 ACT = mybir.ActivationFunctionType
-AXIS = mybir.AxisListType
 
 B, N, C, E = 4, 2048, 1024, 256
 EPS_SUM = 1e-7
@@ -31,8 +30,7 @@ E_BLOCKS = E // P
 
 X_BUFS = 6
 V_LAG = PAIRS_PER_BATCH
-NORM_STEP = PAIRS_PER_BATCH + 5
-G_LAG = 5
+NORM_STEP = PAIRS_PER_BATCH + 4
 LAST_STEP = NORM_STEP + B * PAIRS_PER_BATCH
 
 
@@ -50,8 +48,8 @@ def tile_essattn_pa_t_kernel(tc, x, wk, bk, wv, bv, out_0, out_1):
 
         x_rows, x_t, x_grouped, x_codes, x_scales, k_acc, v_acc = {}, {}, {}, {}, {}, {}, {}
         kb, k_sum, neg_mean, f, f_sum, f_sum_eps, r = {}, {}, {}, {}, {}, {}, {}
-        g_rows, g_t, v_rows, v_grouped = {}, {}, {}, {}
-        norm_parts, norm_sq, norm, r_norm, r_norm_ps, r_norm_rows = {}, {}, {}, {}, {}, {}
+        g_rows, gram, v_rows, v_grouped = {}, {}, {}, {}
+        norm_sq, norm, r_norm, r_norm_ps, r_norm_rows = {}, {}, {}, {}, {}
         v_codes, v_scales, k2_grouped, k2_codes, k2_scales, kv_ps = {}, {}, {}, {}, {}, {}
 
         def load_x(j):
@@ -104,7 +102,7 @@ def tile_essattn_pa_t_kernel(tc, x, wk, bk, wv, bv, out_0, out_1):
         bias = const.tile([P, 2 * E], F32)
         nc.vector.tensor_copy(out=bias[:], in_=bias_bf[:])
 
-        squares = const.tile([P, PACK * P], BF16)
+        masked = const.tile([P, P], F32)
 
         def in_range(j):
             return 0 <= j < PAIRS
@@ -222,38 +220,31 @@ def tile_essattn_pa_t_kernel(tc, x, wk, bk, wv, bv, out_0, out_1):
             r[j] = small.tile([P, PAIR], F32, name="r", tag="r")
             nc.vector.reciprocal(out=r[j][:], in_=f_sum_eps[j][:])
 
-        def normalise_first(j):
+        def normalise(j):
             i, h = divmod(j, PAIRS_PER_GROUP)
             if h == 0:
-                g_rows[i] = stream.tile([P, PACK, E], F32, name="g_rows", tag="g_rows", bufs=7)
-            nc.vector.tensor_scalar_mul(
-                out=g_rows[i][:, h * PAIR, :], in0=f[j][:, 0, :], scalar1=r[j][:, 0:1]
-            )
-
-        def normalise_second(j):
-            i, h = divmod(j, PAIRS_PER_GROUP)
-            nc.scalar.activation(
-                out=g_rows[i][:, h * PAIR + 1, :], in_=f[j][:, 1, :], func=ACT.Copy,
-                scale=r[j][:, 1:2],
-            )
-
-        def transpose_g(i, m):
-            g_t[i, m] = psum.tile([P, PACK, P], F32, name="g_t", tag="g_t")
-            for t in range(PACK):
-                nc.tensor.transpose(g_t[i, m][:, t, :], g_rows[i][:, t, m * P : (m + 1) * P], ident[:])
-
-        def square_norm(i, m):
-            b, grp = divmod(i, GROUPS_PER_BATCH)
-            if grp == 0 and m == 0:
-                norm_parts[b] = small.tile(
-                    [P, E_BLOCKS, GROUPS_PER_BATCH], F32, name="norm_parts", tag="norm_parts", bufs=2
+                g_rows[i] = stream.tile([P, PACK, E], F32, name="g_rows", tag="g_rows", bufs=6)
+            for t in range(PAIR):
+                nc.scalar.activation(
+                    out=g_rows[i][:, h * PAIR + t, :], in_=f[j][:, t, :], func=ACT.Copy,
+                    scale=r[j][:, t : t + 1],
                 )
-            nc.scalar.activation(
-                out=squares[:],
-                in_=g_t[i, m][:].rearrange("p t r -> p (t r)"),
-                func=ACT.Square,
-                accum_out=norm_parts[b][:, m, grp : grp + 1],
-            )
+
+        def multiply_g(j):
+            i, h = divmod(j, PAIRS_PER_GROUP)
+            b, part = divmod(j, PAIRS_PER_BATCH)
+            if part == 0:
+                gram[b] = psum.tile([P, E_BLOCKS, P], F32, name="gram", tag="gram")
+            for t in range(PAIR):
+                for m in range(E_BLOCKS):
+                    block = g_rows[i][:, h * PAIR + t, m * P : (m + 1) * P]
+                    nc.tensor.matmul(
+                        out=gram[b][:, m, :],
+                        lhsT=block,
+                        rhs=block,
+                        start=(part == 0 and t == 0 and m == 0),
+                        stop=(part == PAIRS_PER_BATCH - 1 and t == PAIR - 1 and m == E_BLOCKS - 1),
+                    )
 
         def store_v(i):
             nc.sync.dma_start(out=v_groups[i], in_=v_rows[i][:])
@@ -283,7 +274,16 @@ def tile_essattn_pa_t_kernel(tc, x, wk, bk, wv, bv, out_0, out_1):
 
         def sum_norm(b):
             norm_sq[b] = small.tile([P, E_BLOCKS], F32, name="norm_sq", tag="norm_sq")
-            nc.vector.tensor_reduce(out=norm_sq[b][:], in_=norm_parts[b][:], axis=AXIS.X, op=ALU.add)
+            for m in range(E_BLOCKS):
+                nc.vector.scalar_tensor_tensor(
+                    out=masked[:],
+                    in0=gram[b][:, m, :],
+                    scalar=1.0,
+                    in1=ident[:],
+                    op0=ALU.mult,
+                    op1=ALU.mult,
+                    accum_out=norm_sq[b][:, m : m + 1],
+                )
             nc.vector.tensor_scalar_max(norm_sq[b][:], norm_sq[b][:], EPS_NORM * EPS_NORM)
 
         def root_norm(b):
@@ -361,16 +361,16 @@ def tile_essattn_pa_t_kernel(tc, x, wk, bk, wv, bv, out_0, out_1):
         for s in range(-1, LAST_STEP + 1):
             b, phase = divmod(s - NORM_STEP, PAIRS_PER_BATCH)
             batch_ok = 0 <= b < B
-            g_group, g_block = divmod(s - G_LAG, E_BLOCKS)
-            g_ok = 0 <= g_group < B * GROUPS_PER_BATCH
 
             if in_range(s):
                 quantise_x(s)
+            if batch_ok and phase == 0:
+                sum_norm(b)
             if in_range(s + 1):
                 transpose_x(s + 1)
             load_x(s + 1 + X_BUFS)
-            if g_ok:
-                transpose_g(g_group, g_block)
+            if in_range(s - 4):
+                multiply_g(s - 4)
             if batch_ok and phase == 1:
                 spread_norm(b)
             if in_range(s):
@@ -384,14 +384,11 @@ def tile_essattn_pa_t_kernel(tc, x, wk, bk, wv, bv, out_0, out_1):
                 square_centred(s - 2)
                 add_eps(s - 2)
             if batch_ok and phase == 0:
-                sum_norm(b)
                 root_norm(b)
             if in_range(s + 1):
                 regroup_x(s + 1)
             if in_range(s - 3):
-                normalise_second(s - 3)
-            if g_ok:
-                square_norm(g_group, g_block)
+                normalise(s - 3)
             if batch_ok and phase == 1:
                 copy_norm(b)
             if 0 <= b - 1 and phase == 0:
@@ -412,8 +409,6 @@ def tile_essattn_pa_t_kernel(tc, x, wk, bk, wv, bv, out_0, out_1):
                 quantise_v((s - V_LAG - 2) // PAIRS_PER_GROUP)
             if batch_ok and 3 <= phase < 3 + GROUPS_PER_BATCH:
                 quantise_k2(b, phase - 3)
-            if in_range(s - 2):
-                normalise_first(s - 2)
             if second_of_group(s - V_LAG - 1):
                 round_v((s - V_LAG - 1) // PAIRS_PER_GROUP)
             if batch_ok and 2 <= phase < 2 + GROUPS_PER_BATCH:

@@ -29,8 +29,7 @@ PAIRS = B * PAIRS_PER_BATCH
 E_BLOCKS = E // P
 
 X_BUFS = 6
-V_LAG = PAIRS_PER_BATCH
-NORM_STEP = PAIRS_PER_BATCH + 4
+NORM_STEP = PAIRS_PER_BATCH + 5
 LAST_STEP = NORM_STEP + B * PAIRS_PER_BATCH
 
 
@@ -49,7 +48,7 @@ def tile_essattn_pa_t_kernel(tc, x, wk, bk, wv, bv, out_0, out_1):
         x_rows, x_t, x_grouped, x_codes, x_scales, k_acc, v_acc = {}, {}, {}, {}, {}, {}, {}
         kb, k_sum, neg_mean, f, f_sum, f_sum_eps, r = {}, {}, {}, {}, {}, {}, {}
         g_rows, gram, v_rows, v_grouped = {}, {}, {}, {}
-        norm_sq, norm, r_norm, r_norm_ps, r_norm_rows = {}, {}, {}, {}, {}
+        norm_sq, norm, r_norm, r_norm_rows = {}, {}, {}, {}
         v_codes, v_scales, k2_grouped, k2_codes, k2_scales, kv_ps = {}, {}, {}, {}, {}, {}
 
         def load_x(j):
@@ -133,10 +132,10 @@ def tile_essattn_pa_t_kernel(tc, x, wk, bk, wv, bv, out_0, out_1):
         def quantise_x(j):
             width = PAIR * C // PACK
             x_codes[j] = stream.tile(
-                [P, width], U32, name="x_codes", tag="x_codes", bufs=V_LAG + 2, align_bytes=64
+                [P, width], U32, name="x_codes", tag="x_codes", align_bytes=64
             )
             x_scales[j] = stream.tile(
-                [P, width], U8, name="x_scales", tag="x_scales", bufs=V_LAG + 2, align_bytes=64
+                [P, width], U8, name="x_scales", tag="x_scales", align_bytes=64
             )
             nc.vector.quantize_mx(
                 out=x_codes[j][:].bitcast(FP8X4), scales=x_scales[j][:], in_=x_grouped[j][:]
@@ -259,11 +258,11 @@ def tile_essattn_pa_t_kernel(tc, x, wk, bk, wv, bv, out_0, out_1):
             b, grp = divmod(i, GROUPS_PER_BATCH)
             if grp == 0:
                 v_codes[b] = stream.tile(
-                    [P, GROUPS_PER_BATCH, E], U32, name="v_codes", tag="v_codes",
+                    [P, GROUPS_PER_BATCH, E], U32, name="v_codes", tag="v_codes", bufs=3,
                     align_bytes=64,
                 )
                 v_scales[b] = stream.tile(
-                    [P, GROUPS_PER_BATCH, E], U8, name="v_scales", tag="v_scales",
+                    [P, GROUPS_PER_BATCH, E], U8, name="v_scales", tag="v_scales", bufs=3,
                     align_bytes=64,
                 )
             nc.vector.quantize_mx(
@@ -295,19 +294,15 @@ def tile_essattn_pa_t_kernel(tc, x, wk, bk, wv, bv, out_0, out_1):
             nc.vector.reciprocal(out=r_norm[b][:], in_=norm[b][:])
 
         def spread_norm(b):
-            r_norm_ps[b] = psum.tile([P, E], F32, name="r_norm_ps", tag="batch")
+            r_norm_rows[b] = psum.tile([P, E], F32, name="r_norm_rows", tag="batch")
             for m in range(E_BLOCKS):
                 nc.tensor.matmul(
-                    out=r_norm_ps[b][:, m * P : (m + 1) * P],
+                    out=r_norm_rows[b][:, m * P : (m + 1) * P],
                     lhsT=r_norm[b][:, m : m + 1].to_broadcast([P, P]),
                     rhs=ident[:],
                     start=True,
                     stop=True,
                 )
-
-        def copy_norm(b):
-            r_norm_rows[b] = stream.tile([P, E], F32, name="r_norm_rows", tag="r_norm_rows")
-            nc.scalar.copy(out=r_norm_rows[b][:], in_=r_norm_ps[b][:])
 
         def scale_k2(b, grp):
             i = b * GROUPS_PER_BATCH + grp
@@ -369,14 +364,13 @@ def tile_essattn_pa_t_kernel(tc, x, wk, bk, wv, bv, out_0, out_1):
             if in_range(s + 1):
                 transpose_x(s + 1)
             load_x(s + 1 + X_BUFS)
-            if in_range(s - 4):
-                multiply_g(s - 4)
+            if in_range(s - 5):
+                multiply_g(s - 5)
             if batch_ok and phase == 1:
                 spread_norm(b)
             if in_range(s):
                 project_k(s)
-            if in_range(s - V_LAG):
-                project_v(s - V_LAG)
+                project_v(s)
             if batch_ok and phase == 7:
                 multiply_kv(b)
 
@@ -387,29 +381,26 @@ def tile_essattn_pa_t_kernel(tc, x, wk, bk, wv, bv, out_0, out_1):
                 root_norm(b)
             if in_range(s + 1):
                 regroup_x(s + 1)
-            if in_range(s - 3):
-                normalise(s - 3)
-            if batch_ok and phase == 1:
-                copy_norm(b)
+            if in_range(s - 4):
+                normalise(s - 4)
             if 0 <= b - 1 and phase == 0:
                 store_kv(b - 1)
 
             if in_range(s - 1):
                 add_bias_k(s - 1)
                 negate_mean(s - 1)
-            if in_range(s - V_LAG - 1):
-                add_bias_v(s - V_LAG - 1)
-            if second_of_group(s - V_LAG - 1):
-                store_v((s - V_LAG - 1) // PAIRS_PER_GROUP)
-            if in_range(s - 2):
-                invert_sum(s - 2)
+                add_bias_v(s - 1)
+            if second_of_group(s - 1):
+                store_v((s - 1) // PAIRS_PER_GROUP)
+            if in_range(s - 3):
+                invert_sum(s - 3)
             if batch_ok and phase == 0:
                 invert_norm(b)
-            if second_of_group(s - V_LAG - 2):
-                quantise_v((s - V_LAG - 2) // PAIRS_PER_GROUP)
+            if second_of_group(s - 2):
+                quantise_v((s - 2) // PAIRS_PER_GROUP)
             if batch_ok and 3 <= phase < 3 + GROUPS_PER_BATCH:
                 quantise_k2(b, phase - 3)
-            if second_of_group(s - V_LAG - 1):
-                round_v((s - V_LAG - 1) // PAIRS_PER_GROUP)
+            if second_of_group(s - 1):
+                round_v((s - 1) // PAIRS_PER_GROUP)
             if batch_ok and 2 <= phase < 2 + GROUPS_PER_BATCH:
                 scale_k2(b, phase - 2)

@@ -28,6 +28,7 @@ GROUPS_PER_BATCH = N // K_PASS
 PAIRS = B * PAIRS_PER_BATCH
 E_BLOCKS = E // P
 
+RUN = 4
 X_BUFS = 6
 NORM_STEP = PAIRS_PER_BATCH + 5
 LAST_STEP = NORM_STEP + B * PAIRS_PER_BATCH
@@ -85,8 +86,12 @@ def tile_essattn_pa_t_kernel(tc, x, wk, bk, wv, bv, out_0, out_1):
             for c in range(C_PASSES):
                 for side, rows in enumerate((wk_rows, wv_rows)):
                     nc.vector.tensor_copy(
-                        out=w_grouped[:, c, side * E : (side + 1) * E, :],
-                        in_=rows[:, c * PACK : (c + 1) * PACK, :].rearrange("p t n -> p n t"),
+                        out=w_grouped[:, c, side * E : (side + 1) * E, :].rearrange(
+                            "p (c n) t -> p c t n", n=RUN
+                        ),
+                        in_=rows[:, c * PACK : (c + 1) * PACK, :].rearrange(
+                            "p t (c n) -> p c t n", n=RUN
+                        ),
                     )
             for c in range(C_PASSES):
                 nc.vector.quantize_mx(
@@ -252,7 +257,10 @@ def tile_essattn_pa_t_kernel(tc, x, wk, bk, wv, bv, out_0, out_1):
             v_grouped[i] = stream.tile(
                 [P, E, PACK], BF16, name="v_grouped", tag="v_grouped", align_bytes=64
             )
-            nc.vector.tensor_copy(out=v_grouped[i][:], in_=v_rows[i][:].rearrange("p t e -> p e t"))
+            nc.vector.tensor_copy(
+                out=v_grouped[i][:].rearrange("p (c n) t -> p c t n", n=RUN),
+                in_=v_rows[i][:].rearrange("p t (c n) -> p c t n", n=RUN),
+            )
 
         def quantise_v(i):
             b, grp = divmod(i, GROUPS_PER_BATCH)
@@ -310,9 +318,12 @@ def tile_essattn_pa_t_kernel(tc, x, wk, bk, wv, bv, out_0, out_1):
                 [P, E, PACK], BF16, name="k2_grouped", tag="k2_grouped", align_bytes=64
             )
             nc.vector.tensor_tensor(
-                out=k2_grouped[i][:],
-                in0=g_rows[i][:].rearrange("p t e -> p e t"),
-                in1=r_norm_rows[b][:].unsqueeze(2).to_broadcast([P, E, PACK]),
+                out=k2_grouped[i][:].rearrange("p (c n) t -> p c t n", n=RUN),
+                in0=g_rows[i][:].rearrange("p t (c n) -> p c t n", n=RUN),
+                in1=r_norm_rows[b][:]
+                .rearrange("p (c n) -> p c n", n=RUN)
+                .unsqueeze(2)
+                .to_broadcast([P, E // RUN, PACK, RUN]),
                 op=ALU.mult,
             )
 

@@ -31,7 +31,8 @@ E_BLOCKS = E // P
 RUN = 4
 X_BUFS = 6
 NORM_STEP = PAIRS_PER_BATCH + 5
-LAST_STEP = NORM_STEP + B * PAIRS_PER_BATCH
+KV_PHASE = 6
+LAST_STEP = NORM_STEP + (B - 1) * PAIRS_PER_BATCH + KV_PHASE + 1
 
 
 def tile_essattn_pa_t_kernel(tc, x, wk, bk, wv, bv, out_0, out_1):
@@ -51,6 +52,7 @@ def tile_essattn_pa_t_kernel(tc, x, wk, bk, wv, bv, out_0, out_1):
         g_rows, gram, v_rows, v_grouped = {}, {}, {}, {}
         norm_sq, norm, r_norm, r_norm_rows = {}, {}, {}, {}
         v_codes, v_scales, k2_grouped, k2_codes, k2_scales, kv_ps = {}, {}, {}, {}, {}, {}
+        g_t, g_sq_sums = {}, {}
 
         def load_x(j):
             if j >= PAIRS:
@@ -107,6 +109,7 @@ def tile_essattn_pa_t_kernel(tc, x, wk, bk, wv, bv, out_0, out_1):
         nc.vector.tensor_copy(out=bias[:], in_=bias_bf[:])
 
         masked = const.tile([P, P], F32)
+        squares = const.tile([P, K_PASS], F32)
 
         def in_range(j):
             return 0 <= j < PAIRS
@@ -238,17 +241,16 @@ def tile_essattn_pa_t_kernel(tc, x, wk, bk, wv, bv, out_0, out_1):
             i, h = divmod(j, PAIRS_PER_GROUP)
             b, part = divmod(j, PAIRS_PER_BATCH)
             if part == 0:
-                gram[b] = psum.tile([P, E_BLOCKS, P], F32, name="gram", tag="gram")
+                gram[b] = psum.tile([P, P], F32, name="gram", tag="gram")
             for t in range(PAIR):
-                for m in range(E_BLOCKS):
-                    block = g_rows[i][:, h * PAIR + t, m * P : (m + 1) * P]
-                    nc.tensor.matmul(
-                        out=gram[b][:, m, :],
-                        lhsT=block,
-                        rhs=block,
-                        start=(part == 0 and t == 0 and m == 0),
-                        stop=(part == PAIRS_PER_BATCH - 1 and t == PAIR - 1 and m == E_BLOCKS - 1),
-                    )
+                block = g_rows[i][:, h * PAIR + t, 0:P]
+                nc.tensor.matmul(
+                    out=gram[b][:],
+                    lhsT=block,
+                    rhs=block,
+                    start=(part == 0 and t == 0),
+                    stop=(part == PAIRS_PER_BATCH - 1 and t == PAIR - 1),
+                )
 
         def store_v(i):
             nc.sync.dma_start(out=v_groups[i], in_=v_rows[i][:])
@@ -279,18 +281,38 @@ def tile_essattn_pa_t_kernel(tc, x, wk, bk, wv, bv, out_0, out_1):
                 in_=v_grouped[i][:].rearrange("p e t -> p (e t)"),
             )
 
+        def transpose_g(i):
+            g_t[i] = psum.tile([P, PACK, P], F32, name="g_t", tag="batch")
+            for t in range(PACK):
+                nc.tensor.transpose(g_t[i][:, t, :], g_rows[i][:, t, P:E], ident[:])
+
+        def square_g(i):
+            b, grp = divmod(i, GROUPS_PER_BATCH)
+            if grp == 0:
+                g_sq_sums[b] = small.tile(
+                    [P, GROUPS_PER_BATCH], F32, name="g_sq_sums", tag="g_sq_sums"
+                )
+            nc.scalar.activation(
+                out=squares[:],
+                in_=g_t[i][:].rearrange("p t r -> p (t r)"),
+                func=ACT.Square,
+                accum_out=g_sq_sums[b][:, grp : grp + 1],
+            )
+
         def sum_norm(b):
             norm_sq[b] = small.tile([P, E_BLOCKS], F32, name="norm_sq", tag="norm_sq")
-            for m in range(E_BLOCKS):
-                nc.vector.scalar_tensor_tensor(
-                    out=masked[:],
-                    in0=gram[b][:, m, :],
-                    scalar=1.0,
-                    in1=ident[:],
-                    op0=ALU.mult,
-                    op1=ALU.mult,
-                    accum_out=norm_sq[b][:, m : m + 1],
-                )
+            nc.vector.reduce_sum(
+                out=norm_sq[b][:, 1:2], in_=g_sq_sums[b][:], axis=mybir.AxisListType.X
+            )
+            nc.vector.scalar_tensor_tensor(
+                out=masked[:],
+                in0=gram[b][:],
+                scalar=1.0,
+                in1=ident[:],
+                op0=ALU.mult,
+                op1=ALU.mult,
+                accum_out=norm_sq[b][:, 0:1],
+            )
             nc.vector.tensor_scalar_max(norm_sq[b][:], norm_sq[b][:], EPS_NORM * EPS_NORM)
 
         def root_norm(b):
@@ -302,15 +324,17 @@ def tile_essattn_pa_t_kernel(tc, x, wk, bk, wv, bv, out_0, out_1):
             nc.vector.reciprocal(out=r_norm[b][:], in_=norm[b][:])
 
         def spread_norm(b):
-            r_norm_rows[b] = psum.tile([P, E], F32, name="r_norm_rows", tag="batch")
+            spread = psum.tile([P, E], F32, name="spread", tag="batch")
             for m in range(E_BLOCKS):
                 nc.tensor.matmul(
-                    out=r_norm_rows[b][:, m * P : (m + 1) * P],
+                    out=spread[:, m * P : (m + 1) * P],
                     lhsT=r_norm[b][:, m : m + 1].to_broadcast([P, P]),
                     rhs=ident[:],
                     start=True,
                     stop=True,
                 )
+            r_norm_rows[b] = stream.tile([P, E], F32, name="r_norm_rows", tag="r_norm_rows")
+            nc.scalar.copy(out=r_norm_rows[b][:], in_=spread[:])
 
         def scale_k2(b, grp):
             i = b * GROUPS_PER_BATCH + grp
@@ -372,17 +396,19 @@ def tile_essattn_pa_t_kernel(tc, x, wk, bk, wv, bv, out_0, out_1):
                 quantise_x(s)
             if batch_ok and phase == 0:
                 sum_norm(b)
+            if batch_ok and phase == KV_PHASE + 1:
+                store_kv(b)
             if in_range(s + 1):
                 transpose_x(s + 1)
             load_x(s + 1 + X_BUFS)
+            if second_of_group(s - 5):
+                transpose_g((s - 5) // PAIRS_PER_GROUP)
             if in_range(s - 5):
                 multiply_g(s - 5)
-            if batch_ok and phase == 1:
-                spread_norm(b)
             if in_range(s):
                 project_k(s)
                 project_v(s)
-            if batch_ok and phase == 7:
+            if batch_ok and phase == KV_PHASE:
                 multiply_kv(b)
 
             if in_range(s - 2):
@@ -394,24 +420,26 @@ def tile_essattn_pa_t_kernel(tc, x, wk, bk, wv, bv, out_0, out_1):
                 regroup_x(s + 1)
             if in_range(s - 4):
                 normalise(s - 4)
-            if 0 <= b - 1 and phase == 0:
-                store_kv(b - 1)
+            if second_of_group(s - 5):
+                square_g((s - 5) // PAIRS_PER_GROUP)
 
             if in_range(s - 1):
                 add_bias_k(s - 1)
                 negate_mean(s - 1)
+            if batch_ok and phase == 0:
+                invert_norm(b)
+                spread_norm(b)
+            if in_range(s - 1):
                 add_bias_v(s - 1)
             if second_of_group(s - 1):
                 store_v((s - 1) // PAIRS_PER_GROUP)
             if in_range(s - 3):
                 invert_sum(s - 3)
-            if batch_ok and phase == 0:
-                invert_norm(b)
             if second_of_group(s - 2):
                 quantise_v((s - 2) // PAIRS_PER_GROUP)
-            if batch_ok and 3 <= phase < 3 + GROUPS_PER_BATCH:
-                quantise_k2(b, phase - 3)
+            if batch_ok and 2 <= phase < 2 + GROUPS_PER_BATCH:
+                quantise_k2(b, phase - 2)
             if second_of_group(s - 1):
                 round_v((s - 1) // PAIRS_PER_GROUP)
-            if batch_ok and 2 <= phase < 2 + GROUPS_PER_BATCH:
-                scale_k2(b, phase - 2)
+            if batch_ok and 1 <= phase < 1 + GROUPS_PER_BATCH:
+                scale_k2(b, phase - 1)

@@ -30,10 +30,10 @@ E_BLOCKS = E // P
 
 RUN = 4
 X_BUFS = 6
-NORM_STEP = PAIRS_PER_BATCH + 5
-KV_PHASE = 6
-LAST_STEP = NORM_STEP + (B - 1) * PAIRS_PER_BATCH + KV_PHASE + 1
-
+NORM_STEP = PAIRS_PER_BATCH + 6
+K2_STRIDE = PAIRS_PER_GROUP
+LAST_STEP = NORM_STEP + (B - 1) * PAIRS_PER_BATCH + GROUPS_PER_BATCH + 2
+X_CODE_BUFS = 6
 
 def tile_essattn_pa_t_kernel(tc, x, wk, bk, wv, bv, out_0, out_1):
     nc = tc.nc
@@ -140,10 +140,10 @@ def tile_essattn_pa_t_kernel(tc, x, wk, bk, wv, bv, out_0, out_1):
         def quantise_x(j):
             width = PAIR * C // PACK
             x_codes[j] = stream.tile(
-                [P, width], U32, name="x_codes", tag="x_codes", align_bytes=64
+                [P, width], U32, name="x_codes", tag="x_codes", bufs=X_CODE_BUFS, align_bytes=64
             )
             x_scales[j] = stream.tile(
-                [P, width], U8, name="x_scales", tag="x_scales", align_bytes=64
+                [P, width], U8, name="x_scales", tag="x_scales", bufs=X_CODE_BUFS, align_bytes=64
             )
             nc.vector.quantize_mx(
                 out=x_codes[j][:].bitcast(FP8X4), scales=x_scales[j][:], in_=x_grouped[j][:]
@@ -230,7 +230,7 @@ def tile_essattn_pa_t_kernel(tc, x, wk, bk, wv, bv, out_0, out_1):
         def normalise(j):
             i, h = divmod(j, PAIRS_PER_GROUP)
             if h == 0:
-                g_rows[i] = stream.tile([P, PACK, E], F32, name="g_rows", tag="g_rows", bufs=6)
+                g_rows[i] = stream.tile([P, PACK, E], F32, name="g_rows", tag="g_rows", bufs=8)
             for t in range(PAIR):
                 nc.scalar.activation(
                     out=g_rows[i][:, h * PAIR + t, :], in_=f[j][:, t, :], func=ACT.Copy,
@@ -282,7 +282,7 @@ def tile_essattn_pa_t_kernel(tc, x, wk, bk, wv, bv, out_0, out_1):
             )
 
         def transpose_g(i):
-            g_t[i] = psum.tile([P, PACK, P], F32, name="g_t", tag="batch")
+            g_t[i] = psum.tile([P, PACK, P], F32, name="g_t", tag="v_acc", bufs=2)
             for t in range(PACK):
                 nc.tensor.transpose(g_t[i][:, t, :], g_rows[i][:, t, P:E], ident[:])
 
@@ -324,17 +324,15 @@ def tile_essattn_pa_t_kernel(tc, x, wk, bk, wv, bv, out_0, out_1):
             nc.vector.reciprocal(out=r_norm[b][:], in_=norm[b][:])
 
         def spread_norm(b):
-            spread = psum.tile([P, E], F32, name="spread", tag="batch")
+            r_norm_rows[b] = psum.tile([P, E], F32, name="r_norm_rows", tag="r_norm_rows")
             for m in range(E_BLOCKS):
                 nc.tensor.matmul(
-                    out=spread[:, m * P : (m + 1) * P],
+                    out=r_norm_rows[b][:, m * P : (m + 1) * P],
                     lhsT=r_norm[b][:, m : m + 1].to_broadcast([P, P]),
                     rhs=ident[:],
                     start=True,
                     stop=True,
                 )
-            r_norm_rows[b] = stream.tile([P, E], F32, name="r_norm_rows", tag="r_norm_rows")
-            nc.scalar.copy(out=r_norm_rows[b][:], in_=spread[:])
 
         def scale_k2(b, grp):
             i = b * GROUPS_PER_BATCH + grp
@@ -367,7 +365,7 @@ def tile_essattn_pa_t_kernel(tc, x, wk, bk, wv, bv, out_0, out_1):
             )
 
         def multiply_kv(b):
-            kv_ps[b] = psum.tile([P, E_BLOCKS, E], F32, name="kv_ps", tag="batch")
+            kv_ps[b] = psum.tile([P, E_BLOCKS, E], F32, name="kv_ps", tag="v_acc", bufs=2)
             for m in range(E_BLOCKS):
                 for grp in range(GROUPS_PER_BATCH):
                     nc.tensor.matmul_mx(
@@ -388,58 +386,76 @@ def tile_essattn_pa_t_kernel(tc, x, wk, bk, wv, bv, out_0, out_1):
         def second_of_group(j):
             return in_range(j) and j % PAIRS_PER_GROUP == PAIRS_PER_GROUP - 1
 
+        v_pair = {j: j for j in range(PAIRS)}
+
+        k2_steps = {}
+
+        def at(step, what, item):
+            k2_steps.setdefault(step, ([], [], [], []))[what].append(item)
+
+        for b in range(B):
+            stride = K2_STRIDE if b < B - 1 else 1
+            for grp in range(GROUPS_PER_BATCH):
+                step = NORM_STEP + b * PAIRS_PER_BATCH + 1 + grp * stride
+                at(step, 0, b * GROUPS_PER_BATCH + grp)
+                at(step + 1, 1, b * GROUPS_PER_BATCH + grp)
+            at(step + 1, 2, b)
+            at(step + 2, 3, b)
+
         for s in range(-1, LAST_STEP + 1):
+            v_now, v_one, v_two = (v_pair.get(s - d, -1) for d in range(3))
             b, phase = divmod(s - NORM_STEP, PAIRS_PER_BATCH)
-            batch_ok = 0 <= b < B
+            scale_now, quantise_now, multiply_now, store_now = k2_steps.get(s, ([], [], [], []))
 
             if in_range(s):
                 quantise_x(s)
-            if batch_ok and phase == 0:
+            if 0 <= b < B and phase == 0:
                 sum_norm(b)
-            if batch_ok and phase == KV_PHASE + 1:
-                store_kv(b)
+            if in_range(v_one):
+                add_bias_v(v_one)
+            if second_of_group(v_one):
+                store_v(v_one // PAIRS_PER_GROUP)
             if in_range(s + 1):
                 transpose_x(s + 1)
             load_x(s + 1 + X_BUFS)
-            if second_of_group(s - 5):
-                transpose_g((s - 5) // PAIRS_PER_GROUP)
-            if in_range(s - 5):
-                multiply_g(s - 5)
+            if second_of_group(s - 6):
+                transpose_g((s - 6) // PAIRS_PER_GROUP)
+            if in_range(s - 6):
+                multiply_g(s - 6)
             if in_range(s):
                 project_k(s)
-                project_v(s)
-            if batch_ok and phase == KV_PHASE:
-                multiply_kv(b)
+            if in_range(v_now):
+                project_v(v_now)
 
             if in_range(s - 2):
                 square_centred(s - 2)
                 add_eps(s - 2)
-            if batch_ok and phase == 0:
+            if 0 <= b < B and phase == 0:
                 root_norm(b)
             if in_range(s + 1):
                 regroup_x(s + 1)
             if in_range(s - 4):
                 normalise(s - 4)
-            if second_of_group(s - 5):
-                square_g((s - 5) // PAIRS_PER_GROUP)
+            if second_of_group(s - 6):
+                square_g((s - 6) // PAIRS_PER_GROUP)
+            for i in store_now:
+                store_kv(i)
 
             if in_range(s - 1):
                 add_bias_k(s - 1)
                 negate_mean(s - 1)
-            if batch_ok and phase == 0:
+            if 0 <= b < B and phase == 0:
                 invert_norm(b)
                 spread_norm(b)
-            if in_range(s - 1):
-                add_bias_v(s - 1)
-            if second_of_group(s - 1):
-                store_v((s - 1) // PAIRS_PER_GROUP)
             if in_range(s - 3):
                 invert_sum(s - 3)
-            if second_of_group(s - 2):
-                quantise_v((s - 2) // PAIRS_PER_GROUP)
-            if batch_ok and 2 <= phase < 2 + GROUPS_PER_BATCH:
-                quantise_k2(b, phase - 2)
-            if second_of_group(s - 1):
-                round_v((s - 1) // PAIRS_PER_GROUP)
-            if batch_ok and 1 <= phase < 1 + GROUPS_PER_BATCH:
-                scale_k2(b, phase - 1)
+            for i in quantise_now:
+                quantise_k2(*divmod(i, GROUPS_PER_BATCH))
+            for i in multiply_now:
+                multiply_kv(i)
+            if second_of_group(v_two):
+                quantise_v(v_two // PAIRS_PER_GROUP)
+            if second_of_group(v_one):
+                round_v(v_one // PAIRS_PER_GROUP)
+            for i in scale_now:
+                scale_k2(*divmod(i, GROUPS_PER_BATCH))

@@ -48,7 +48,7 @@ def tile_essattn_pa_t_kernel(tc, x, wk, bk, wv, bv, out_0, out_1):
         psum = ctx.enter_context(tc.psum_pool(name="psum", bufs=1))
 
         x_rows, x_t, x_grouped, x_codes, x_scales, k_acc, v_acc = {}, {}, {}, {}, {}, {}, {}
-        kb, k_sum, neg_mean, f, f_sum, f_sum_eps, r = {}, {}, {}, {}, {}, {}, {}
+        kb, neg_mean, f, f_sum, f_sum_eps, r = {}, {}, {}, {}, {}, {}
         g_rows, gram, v_rows, v_grouped = {}, {}, {}, {}
         norm_sq, norm, r_norm, r_norm_rows = {}, {}, {}, {}
         v_codes, v_scales, k2_grouped, k2_codes, k2_scales, kv_ps = {}, {}, {}, {}, {}, {}
@@ -69,44 +69,64 @@ def tile_essattn_pa_t_kernel(tc, x, wk, bk, wv, bv, out_0, out_1):
 
         one = const.tile([P, 1], F32)
         nc.vector.memset(one[:], 1.0)
+        minus_one = const.tile([P, PAIR], F32)
+        nc.gpsimd.memset(minus_one[:], -1.0)
         sqrt_one = const.tile([P, 1], F32)
         nc.scalar.sqrt(sqrt_one[:], one[:])
 
-        w_codes = const.tile([P, C_PASSES, 2 * E], U32, align_bytes=64)
-        w_scales = const.tile([P, C_PASSES, 2 * E], U8, align_bytes=64)
-        with tc.tile_pool(name="w_stage", bufs=1) as w_stage:
-            wk_rows = w_stage.tile([P, C_PASSES * PACK, E], BF16)
-            wv_rows = w_stage.tile([P, C_PASSES * PACK, E], BF16)
-            for rows, w in ((wk_rows, wk), (wv_rows, wv)):
-                nc.sync.dma_start(
-                    out=rows[:].rearrange("p (h e) n -> p h (e n)", e=2),
-                    in_=w.rearrange("(h p e) n -> p h (e n)", p=P, e=2),
-                )
-            for j in range(X_BUFS):
-                load_x(j)
-            w_grouped = w_stage.tile([P, C_PASSES, 2 * E, PACK], BF16, align_bytes=64)
-            for c in range(C_PASSES):
-                for side, rows in enumerate((wk_rows, wv_rows)):
-                    nc.vector.tensor_copy(
-                        out=w_grouped[:, c, side * E : (side + 1) * E, :].rearrange(
-                            "p (c n) t -> p c t n", n=RUN
-                        ),
-                        in_=rows[:, c * PACK : (c + 1) * PACK, :].rearrange(
-                            "p t (c n) -> p c t n", n=RUN
-                        ),
-                    )
-            for c in range(C_PASSES):
-                nc.vector.quantize_mx(
-                    out=w_codes[:, c, :].bitcast(FP8X4),
-                    scales=w_scales[:, c, :],
-                    in_=w_grouped[:, c].rearrange("p n t -> p (n t)"),
-                )
+        bias_row = const.tile([P, 2 * E], BF16)
+        nc.gpsimd.memset(bias_row[:], 0.0)
+        nc.scalar.dma_start(out=bias_row[0:1, 0:E], in_=bk.unsqueeze(0))
+        nc.scalar.dma_start(out=bias_row[0:1, E : 2 * E], in_=bv.unsqueeze(0))
+        ones = const.tile([P, P], BF16)
+        nc.vector.memset(ones[:], 1.0)
 
-        bias_bf = const.tile([P, 2 * E], BF16)
-        nc.scalar.dma_start(out=bias_bf[:, 0:E], in_=bk.partition_broadcast(P))
-        nc.scalar.dma_start(out=bias_bf[:, E : 2 * E], in_=bv.partition_broadcast(P))
+        w_codes = const.tile([P, 2, C_PASSES, E], U32, align_bytes=64)
+        w_scales = const.tile([P, 2, C_PASSES, E], U8, align_bytes=64)
+        w_stage = ctx.enter_context(tc.tile_pool(name="w_stage", bufs=1))
+        w_grouped = w_stage.tile([P, 2, C_PASSES, E, PACK], BF16, align_bytes=64)
+        w_rows = []
+        for side, w in enumerate((wk, wv)):
+            rows = w_stage.tile([P, C_PASSES * PACK, E], BF16, name="w_rows", tag="w_rows", bufs=2)
+            nc.sync.dma_start(
+                out=rows[:].rearrange("p (h e) n -> p h (e n)", e=2),
+                in_=w.rearrange("(h p e) n -> p h (e n)", p=P, e=2),
+            )
+            w_rows.append(rows)
+            if side == 0:
+                load_x(0)
+        for j in range(1, X_BUFS):
+            load_x(j)
+
+        def regroup_w(side, c, copy):
+            copy(
+                out=w_grouped[:, side, c].rearrange("p (d n) t -> p d t n", n=RUN),
+                in_=w_rows[side][:, c * PACK : (c + 1) * PACK, :].rearrange(
+                    "p t (d n) -> p d t n", n=RUN
+                ),
+            )
+
+        def quantise_w(side):
+            nc.vector.quantize_mx(
+                out=w_codes[:, side].rearrange("p c n -> p (c n)").bitcast(FP8X4),
+                scales=w_scales[:, side].rearrange("p c n -> p (c n)"),
+                in_=w_grouped[:, side].rearrange("p c n t -> p (c n t)"),
+            )
+
+        regroup_w(0, 0, nc.vector.tensor_copy)
+        regroup_w(0, 1, nc.scalar.copy)
+        quantise_w(0)
+
         bias = const.tile([P, 2 * E], F32)
-        nc.vector.tensor_copy(out=bias[:], in_=bias_bf[:])
+
+        def spread_bias():
+            rows = psum.tile([P, 2 * E], F32, name="bias_rows", tag="gram")
+            nc.tensor.matmul(out=rows[:], lhsT=ones[:], rhs=bias_row[:], start=True, stop=True)
+            nc.vector.tensor_scalar(
+                out=bias[:, 0:E], in0=rows[:, 0:E], scalar1=-1.0 / E, scalar2=0.0,
+                op0=ALU.mult, op1=ALU.add,
+            )
+            nc.vector.tensor_copy(out=bias[:, E : 2 * E], in_=rows[:, E : 2 * E])
 
         masked = const.tile([P, P], F32)
         squares = const.tile([P, K_PASS], F32)
@@ -157,8 +177,8 @@ def tile_essattn_pa_t_kernel(tc, x, wk, bk, wv, bv, out_0, out_1):
                         out=bank[:, t, :],
                         lhsT=x_codes[j][:, cols].bitcast(FP8X4),
                         lhsT_scale=x_scales[j][:, cols],
-                        rhs=w_codes[:, c, side * E : (side + 1) * E].bitcast(FP8X4),
-                        rhs_scale=w_scales[:, c, side * E : (side + 1) * E],
+                        rhs=w_codes[:, side, c, :].bitcast(FP8X4),
+                        rhs_scale=w_scales[:, side, c, :],
                         start=(c == 0),
                         stop=(c == C_PASSES - 1),
                     )
@@ -173,16 +193,16 @@ def tile_essattn_pa_t_kernel(tc, x, wk, bk, wv, bv, out_0, out_1):
 
         def add_bias_k(j):
             kb[j] = stream.tile([P, PAIR, E], F32, name="kb", tag="kb")
-            k_sum[j] = small.tile([P, PAIR], F32, name="k_sum", tag="k_sum")
+            neg_mean[j] = small.tile([P, PAIR], F32, name="neg_mean", tag="neg_mean")
             for t in range(PAIR):
                 nc.vector.scalar_tensor_tensor(
                     out=kb[j][:, t, :],
                     in0=k_acc[j][:, t, :],
-                    scalar=1.0,
+                    scalar=-1.0 / E,
                     in1=bias[:, 0:E],
                     op0=ALU.mult,
                     op1=ALU.add,
-                    accum_out=k_sum[j][:, t : t + 1],
+                    accum_out=neg_mean[j][:, t : t + 1],
                 )
 
         def add_bias_v(j):
@@ -196,13 +216,6 @@ def tile_essattn_pa_t_kernel(tc, x, wk, bk, wv, bv, out_0, out_1):
                 op=ALU.add,
             )
 
-        def negate_mean(j):
-            neg_mean[j] = small.tile([P, PAIR], F32, name="neg_mean", tag="neg_mean")
-            nc.gpsimd.tensor_scalar(
-                out=neg_mean[j][:], in0=k_sum[j][:], scalar1=-1.0 / E, scalar2=0.0,
-                op0=ALU.mult, op1=ALU.add,
-            )
-
         def square_centred(j):
             f[j] = stream.tile([P, PAIR, E], F32, name="f", tag="f", bufs=3)
             f_sum[j] = small.tile([P, PAIR], F32, name="f_sum", tag="f_sum")
@@ -212,7 +225,7 @@ def tile_essattn_pa_t_kernel(tc, x, wk, bk, wv, bv, out_0, out_1):
                     in_=kb[j][:, t, :],
                     func=ACT.Square,
                     bias=neg_mean[j][:, t : t + 1],
-                    scale=1.0,
+                    scale=-float(E),
                     accum_out=f_sum[j][:, t : t + 1],
                 )
 
@@ -225,7 +238,9 @@ def tile_essattn_pa_t_kernel(tc, x, wk, bk, wv, bv, out_0, out_1):
 
         def invert_sum(j):
             r[j] = small.tile([P, PAIR], F32, name="r", tag="r")
-            nc.vector.reciprocal(out=r[j][:], in_=f_sum_eps[j][:])
+            nc.gpsimd.tensor_tensor(
+                out=r[j][:], in0=f_sum_eps[j][:], in1=minus_one[:], op=ALU.pow
+            )
 
         def normalise(j):
             i, h = divmod(j, PAIRS_PER_GROUP)
@@ -424,12 +439,18 @@ def tile_essattn_pa_t_kernel(tc, x, wk, bk, wv, bv, out_0, out_1):
                 multiply_g(s - 6)
             if in_range(s):
                 project_k(s)
+            if s == 0:
+                for c in range(C_PASSES):
+                    regroup_w(1, c, nc.vector.tensor_copy)
+                quantise_w(1)
+                spread_bias()
             if in_range(v_now):
                 project_v(v_now)
 
             if in_range(s - 2):
                 square_centred(s - 2)
                 add_eps(s - 2)
+                invert_sum(s - 2)
             if 0 <= b < B and phase == 0:
                 root_norm(b)
             if in_range(s + 1):
@@ -443,12 +464,9 @@ def tile_essattn_pa_t_kernel(tc, x, wk, bk, wv, bv, out_0, out_1):
 
             if in_range(s - 1):
                 add_bias_k(s - 1)
-                negate_mean(s - 1)
             if 0 <= b < B and phase == 0:
                 invert_norm(b)
                 spread_norm(b)
-            if in_range(s - 3):
-                invert_sum(s - 3)
             for i in quantise_now:
                 quantise_k2(*divmod(i, GROUPS_PER_BATCH))
             for i in multiply_now:

@@ -32,7 +32,7 @@ RUN = 4
 X_BUFS = 6
 NORM_STEP = PAIRS_PER_BATCH + 6
 K2_STRIDE = PAIRS_PER_GROUP
-LAST_STEP = NORM_STEP + (B - 1) * PAIRS_PER_BATCH + GROUPS_PER_BATCH + 2
+LAST_STEP = NORM_STEP + (B - 1) * PAIRS_PER_BATCH
 X_CODE_BUFS = 6
 
 def tile_essattn_pa_t_kernel(tc, x, wk, bk, wv, bv, out_0, out_1):
@@ -69,8 +69,6 @@ def tile_essattn_pa_t_kernel(tc, x, wk, bk, wv, bv, out_0, out_1):
 
         one = const.tile([P, 1], F32)
         nc.vector.memset(one[:], 1.0)
-        minus_one = const.tile([P, PAIR], F32)
-        nc.gpsimd.memset(minus_one[:], -1.0)
         sqrt_one = const.tile([P, 1], F32)
         nc.scalar.sqrt(sqrt_one[:], one[:])
 
@@ -122,11 +120,8 @@ def tile_essattn_pa_t_kernel(tc, x, wk, bk, wv, bv, out_0, out_1):
         def spread_bias():
             rows = psum.tile([P, 2 * E], F32, name="bias_rows", tag="gram")
             nc.tensor.matmul(out=rows[:], lhsT=ones[:], rhs=bias_row[:], start=True, stop=True)
-            nc.vector.tensor_scalar(
-                out=bias[:, 0:E], in0=rows[:, 0:E], scalar1=-1.0 / E, scalar2=0.0,
-                op0=ALU.mult, op1=ALU.add,
-            )
-            nc.vector.tensor_copy(out=bias[:, E : 2 * E], in_=rows[:, E : 2 * E])
+            nc.scalar.mul(bias[:, 0:E], rows[:, 0:E], -1.0 / E)
+            nc.scalar.copy(out=bias[:, E : 2 * E], in_=rows[:, E : 2 * E])
 
         masked = const.tile([P, P], F32)
         squares = const.tile([P, K_PASS], F32)
@@ -238,9 +233,7 @@ def tile_essattn_pa_t_kernel(tc, x, wk, bk, wv, bv, out_0, out_1):
 
         def invert_sum(j):
             r[j] = small.tile([P, PAIR], F32, name="r", tag="r")
-            nc.gpsimd.tensor_tensor(
-                out=r[j][:], in0=f_sum_eps[j][:], in1=minus_one[:], op=ALU.pow
-            )
+            nc.vector.reciprocal(out=r[j][:], in_=f_sum_eps[j][:])
 
         def normalise(j):
             i, h = divmod(j, PAIRS_PER_GROUP)
@@ -349,15 +342,15 @@ def tile_essattn_pa_t_kernel(tc, x, wk, bk, wv, bv, out_0, out_1):
                     stop=True,
                 )
 
-        def scale_k2(b, grp):
+        def scale_k2(b, grp, engine, row):
             i = b * GROUPS_PER_BATCH + grp
             k2_grouped[i] = stream.tile(
-                [P, E, PACK], BF16, name="k2_grouped", tag="k2_grouped", align_bytes=64
+                [P, E, PACK], BF16, name="k2_grouped", tag="k2_grouped", bufs=4, align_bytes=64
             )
-            nc.vector.tensor_tensor(
+            engine.tensor_tensor(
                 out=k2_grouped[i][:].rearrange("p (c n) t -> p c t n", n=RUN),
                 in0=g_rows[i][:].rearrange("p t (c n) -> p c t n", n=RUN),
-                in1=r_norm_rows[b][:]
+                in1=row[:]
                 .rearrange("p (c n) -> p c n", n=RUN)
                 .unsqueeze(2)
                 .to_broadcast([P, E // RUN, PACK, RUN]),
@@ -379,19 +372,22 @@ def tile_essattn_pa_t_kernel(tc, x, wk, bk, wv, bv, out_0, out_1):
                 in_=k2_grouped[i][:].rearrange("p e t -> p (e t)"),
             )
 
+        def multiply_kv_group(b, grp, m, out):
+            nc.tensor.matmul_mx(
+                out=out,
+                lhsT=k2_codes[b][:, grp, m * P : (m + 1) * P].bitcast(FP8X4),
+                lhsT_scale=k2_scales[b][:, grp, m * P : (m + 1) * P],
+                rhs=v_codes[b][:, grp, :].bitcast(FP8X4),
+                rhs_scale=v_scales[b][:, grp, :],
+                start=(grp == 0),
+                stop=(grp == GROUPS_PER_BATCH - 1),
+            )
+
         def multiply_kv(b):
             kv_ps[b] = psum.tile([P, E_BLOCKS, E], F32, name="kv_ps", tag="v_acc", bufs=2)
             for m in range(E_BLOCKS):
                 for grp in range(GROUPS_PER_BATCH):
-                    nc.tensor.matmul_mx(
-                        out=kv_ps[b][:, m, :],
-                        lhsT=k2_codes[b][:, grp, m * P : (m + 1) * P].bitcast(FP8X4),
-                        lhsT_scale=k2_scales[b][:, grp, m * P : (m + 1) * P],
-                        rhs=v_codes[b][:, grp, :].bitcast(FP8X4),
-                        rhs_scale=v_scales[b][:, grp, :],
-                        start=(grp == 0),
-                        stop=(grp == GROUPS_PER_BATCH - 1),
-                    )
+                    multiply_kv_group(b, grp, m, kv_ps[b][:, m, :])
 
         def store_kv(b):
             kv_rows = stream.tile([P, E_BLOCKS, E], F32, name="kv_rows", tag="kv_rows")
@@ -408,10 +404,9 @@ def tile_essattn_pa_t_kernel(tc, x, wk, bk, wv, bv, out_0, out_1):
         def at(step, what, item):
             k2_steps.setdefault(step, ([], [], [], []))[what].append(item)
 
-        for b in range(B):
-            stride = K2_STRIDE if b < B - 1 else 1
+        for b in range(B - 1):
             for grp in range(GROUPS_PER_BATCH):
-                step = NORM_STEP + b * PAIRS_PER_BATCH + 1 + grp * stride
+                step = NORM_STEP + b * PAIRS_PER_BATCH + 1 + grp * K2_STRIDE
                 at(step, 0, b * GROUPS_PER_BATCH + grp)
                 at(step + 1, 1, b * GROUPS_PER_BATCH + grp)
             at(step + 1, 2, b)
@@ -443,18 +438,18 @@ def tile_essattn_pa_t_kernel(tc, x, wk, bk, wv, bv, out_0, out_1):
                 for c in range(C_PASSES):
                     regroup_w(1, c, nc.vector.tensor_copy)
                 quantise_w(1)
-                spread_bias()
             if in_range(v_now):
                 project_v(v_now)
 
             if in_range(s - 2):
                 square_centred(s - 2)
                 add_eps(s - 2)
-                invert_sum(s - 2)
             if 0 <= b < B and phase == 0:
                 root_norm(b)
             if in_range(s + 1):
                 regroup_x(s + 1)
+            if s == 0:
+                spread_bias()
             if in_range(s - 4):
                 normalise(s - 4)
             if second_of_group(s - 6):
@@ -467,6 +462,8 @@ def tile_essattn_pa_t_kernel(tc, x, wk, bk, wv, bv, out_0, out_1):
             if 0 <= b < B and phase == 0:
                 invert_norm(b)
                 spread_norm(b)
+            if in_range(s - 3):
+                invert_sum(s - 3)
             for i in quantise_now:
                 quantise_k2(*divmod(i, GROUPS_PER_BATCH))
             for i in multiply_now:
@@ -476,4 +473,30 @@ def tile_essattn_pa_t_kernel(tc, x, wk, bk, wv, bv, out_0, out_1):
             if second_of_group(v_one):
                 round_v(v_one // PAIRS_PER_GROUP)
             for i in scale_now:
-                scale_k2(*divmod(i, GROUPS_PER_BATCH))
+                b_k2, grp = divmod(i, GROUPS_PER_BATCH)
+                scale_k2(b_k2, grp, nc.vector, r_norm_rows[b_k2])
+
+        last = B - 1
+        groups = range(GROUPS_PER_BATCH)
+        r_norm_sbuf = const.tile([P, E], F32)
+        nc.scalar.copy(out=r_norm_sbuf[:], in_=r_norm_rows[last][:])
+        for grp in groups:
+            if grp == GROUPS_PER_BATCH - 1:
+                scale_k2(last, grp, nc.gpsimd, r_norm_sbuf)
+            else:
+                scale_k2(last, grp, nc.vector, r_norm_rows[last])
+        store_kv(last - 1)
+        kv_banks = [
+            psum.tile([P, E], F32, name="kv_bank", tag=tag, bufs=2) for tag in ("v_acc", "k_acc")
+        ]
+        for grp in groups:
+            quantise_k2(last, grp)
+            for m, bank in enumerate(kv_banks):
+                multiply_kv_group(last, grp, m, bank[:])
+        for bank, m, copy, queue in (
+            (kv_banks[0], 0, nc.scalar.copy, nc.sync),
+            (kv_banks[1], 1, nc.vector.tensor_copy, nc.scalar),
+        ):
+            rows = stream.tile([P, E], F32, name="kv_block", tag="kv_block")
+            copy(out=rows[:], in_=bank[:])
+            queue.dma_start(out=out_0[last][m * P : (m + 1) * P, :], in_=rows[:])

@@ -29,6 +29,7 @@ PAIRS = B * PAIRS_PER_BATCH
 E_BLOCKS = E // P
 
 RUN = 4
+ROUND_PARTS = 2
 X_BUFS = 6
 NORM_STEP = PAIRS_PER_BATCH + 6
 K2_STRIDE = PAIRS_PER_GROUP
@@ -263,13 +264,19 @@ def tile_essattn_pa_t_kernel(tc, x, wk, bk, wv, bv, out_0, out_1):
         def store_v(i):
             nc.sync.dma_start(out=v_groups[i], in_=v_rows[i][:])
 
-        def round_v(i):
-            v_grouped[i] = stream.tile(
-                [P, E, PACK], BF16, name="v_grouped", tag="v_grouped", align_bytes=64
-            )
-            nc.vector.tensor_copy(
-                out=v_grouped[i][:].rearrange("p (c n) t -> p c t n", n=RUN),
-                in_=v_rows[i][:].rearrange("p t (c n) -> p c t n", n=RUN),
+        def round_v(i, part):
+            if part == 0:
+                v_grouped[i] = stream.tile(
+                    [P, E, PACK], BF16, name="v_grouped", tag="v_grouped", align_bytes=64
+                )
+            cols = slice(part * E // ROUND_PARTS, (part + 1) * E // ROUND_PARTS)
+            nc.gpsimd.tensor_scalar(
+                out=v_grouped[i][:, cols, :],
+                in0=v_rows[i][:, :, cols].rearrange("p t e -> p e t"),
+                scalar1=1.0,
+                scalar2=0.0,
+                op0=ALU.mult,
+                op1=ALU.add,
             )
 
         def quantise_v(i):
@@ -413,7 +420,7 @@ def tile_essattn_pa_t_kernel(tc, x, wk, bk, wv, bv, out_0, out_1):
             at(step + 2, 3, b)
 
         for s in range(-1, LAST_STEP + 1):
-            v_now, v_one, v_two = (v_pair.get(s - d, -1) for d in range(3))
+            v_now, v_one, v_two, v_three = (v_pair.get(s - d, -1) for d in range(4))
             b, phase = divmod(s - NORM_STEP, PAIRS_PER_BATCH)
             scale_now, quantise_now, multiply_now, store_now = k2_steps.get(s, ([], [], [], []))
 
@@ -444,6 +451,12 @@ def tile_essattn_pa_t_kernel(tc, x, wk, bk, wv, bv, out_0, out_1):
             if in_range(s - 2):
                 square_centred(s - 2)
                 add_eps(s - 2)
+            if second_of_group(v_one):
+                for part in range(1):
+                    round_v(v_one // PAIRS_PER_GROUP, part)
+            if second_of_group(v_two):
+                for part in range(1, ROUND_PARTS):
+                    round_v(v_two // PAIRS_PER_GROUP, part)
             if 0 <= b < B and phase == 0:
                 root_norm(b)
             if in_range(s + 1):
@@ -468,10 +481,8 @@ def tile_essattn_pa_t_kernel(tc, x, wk, bk, wv, bv, out_0, out_1):
                 quantise_k2(*divmod(i, GROUPS_PER_BATCH))
             for i in multiply_now:
                 multiply_kv(i)
-            if second_of_group(v_two):
-                quantise_v(v_two // PAIRS_PER_GROUP)
-            if second_of_group(v_one):
-                round_v(v_one // PAIRS_PER_GROUP)
+            if second_of_group(v_three):
+                quantise_v(v_three // PAIRS_PER_GROUP)
             for i in scale_now:
                 b_k2, grp = divmod(i, GROUPS_PER_BATCH)
                 scale_k2(b_k2, grp, nc.vector, r_norm_rows[b_k2])

@@ -29,7 +29,7 @@ PAIRS = B * PAIRS_PER_BATCH
 E_BLOCKS = E // P
 
 RUN = 4
-ROUND_PARTS = 2
+ROUND_PARTS = 4
 X_BUFS = 6
 NORM_STEP = PAIRS_PER_BATCH + 6
 K2_STRIDE = PAIRS_PER_GROUP
@@ -271,8 +271,8 @@ def tile_essattn_pa_t_kernel(tc, x, wk, bk, wv, bv, out_0, out_1):
                 )
             cols = slice(part * E // ROUND_PARTS, (part + 1) * E // ROUND_PARTS)
             nc.gpsimd.tensor_scalar(
-                out=v_grouped[i][:, cols, :],
-                in0=v_rows[i][:, :, cols].rearrange("p t e -> p e t"),
+                out=v_grouped[i][:, cols, :].rearrange("p (c n) t -> p c t n", n=RUN),
+                in0=v_rows[i][:, :, cols].rearrange("p t (c n) -> p c t n", n=RUN),
                 scalar1=1.0,
                 scalar2=0.0,
                 op0=ALU.mult,
@@ -435,10 +435,10 @@ def tile_essattn_pa_t_kernel(tc, x, wk, bk, wv, bv, out_0, out_1):
             if in_range(s + 1):
                 transpose_x(s + 1)
             load_x(s + 1 + X_BUFS)
-            if second_of_group(s - 6):
-                transpose_g((s - 6) // PAIRS_PER_GROUP)
             if in_range(s - 6):
                 multiply_g(s - 6)
+            if second_of_group(s - 6):
+                transpose_g((s - 6) // PAIRS_PER_GROUP)
             if in_range(s):
                 project_k(s)
             if s == 0:

@@ -74,9 +74,9 @@ def tile_essattn_pa_t_kernel(tc, x, wk, bk, wv, bv, out_0, out_1):
         nc.scalar.sqrt(sqrt_one[:], one[:])
 
         bias_row = const.tile([P, 2 * E], BF16)
-        nc.gpsimd.memset(bias_row[:], 0.0)
-        nc.scalar.dma_start(out=bias_row[0:1, 0:E], in_=bk.unsqueeze(0))
-        nc.scalar.dma_start(out=bias_row[0:1, E : 2 * E], in_=bv.unsqueeze(0))
+        nc.vector.memset(bias_row[:], 0.0)
+        nc.sync.dma_start(out=bias_row[0:1, 0:E], in_=bk.unsqueeze(0))
+        nc.sync.dma_start(out=bias_row[0:1, E : 2 * E], in_=bv.unsqueeze(0))
         ones = const.tile([P, P], BF16)
         nc.vector.memset(ones[:], 1.0)
 
@@ -112,17 +112,15 @@ def tile_essattn_pa_t_kernel(tc, x, wk, bk, wv, bv, out_0, out_1):
                 in_=w_grouped[:, side].rearrange("p c n t -> p (c n t)"),
             )
 
+        bias = const.tile([P, 2 * E], F32)
+        bias_rows = psum.tile([P, 2 * E], F32, name="bias_rows", tag="gram")
+        nc.tensor.matmul(out=bias_rows[:], lhsT=ones[:], rhs=bias_row[:], start=True, stop=True)
+        nc.scalar.mul(bias[:, 0:E], bias_rows[:, 0:E], -1.0 / E)
+        nc.scalar.copy(out=bias[:, E : 2 * E], in_=bias_rows[:, E : 2 * E])
+
         regroup_w(0, 0, nc.vector.tensor_copy)
         regroup_w(0, 1, nc.scalar.copy)
         quantise_w(0)
-
-        bias = const.tile([P, 2 * E], F32)
-
-        def spread_bias():
-            rows = psum.tile([P, 2 * E], F32, name="bias_rows", tag="gram")
-            nc.tensor.matmul(out=rows[:], lhsT=ones[:], rhs=bias_row[:], start=True, stop=True)
-            nc.scalar.mul(bias[:, 0:E], rows[:, 0:E], -1.0 / E)
-            nc.scalar.copy(out=bias[:, E : 2 * E], in_=rows[:, E : 2 * E])
 
         masked = const.tile([P, P], F32)
         squares = const.tile([P, K_PASS], F32)
@@ -426,8 +424,6 @@ def tile_essattn_pa_t_kernel(tc, x, wk, bk, wv, bv, out_0, out_1):
 
             if in_range(s):
                 quantise_x(s)
-            if 0 <= b < B and phase == 0:
-                sum_norm(b)
             if in_range(v_one):
                 add_bias_v(v_one)
             if second_of_group(v_one):
@@ -435,19 +431,18 @@ def tile_essattn_pa_t_kernel(tc, x, wk, bk, wv, bv, out_0, out_1):
             if in_range(s + 1):
                 transpose_x(s + 1)
             load_x(s + 1 + X_BUFS)
-            if in_range(s - 6):
-                multiply_g(s - 6)
             if second_of_group(s - 6):
                 transpose_g((s - 6) // PAIRS_PER_GROUP)
             if in_range(s):
                 project_k(s)
             if s == 0:
-                for c in range(C_PASSES):
-                    regroup_w(1, c, nc.vector.tensor_copy)
+                regroup_w(1, 0, nc.vector.tensor_copy)
+                regroup_w(1, 1, nc.scalar.copy)
                 quantise_w(1)
             if in_range(v_now):
                 project_v(v_now)
-
+            if in_range(s - 6):
+                multiply_g(s - 6)
             if in_range(s - 2):
                 square_centred(s - 2)
                 add_eps(s - 2)
@@ -458,18 +453,17 @@ def tile_essattn_pa_t_kernel(tc, x, wk, bk, wv, bv, out_0, out_1):
                 for part in range(1, ROUND_PARTS):
                     round_v(v_two // PAIRS_PER_GROUP, part)
             if 0 <= b < B and phase == 0:
+                sum_norm(b)
+            if 0 <= b < B and phase == 0:
                 root_norm(b)
             if in_range(s + 1):
                 regroup_x(s + 1)
-            if s == 0:
-                spread_bias()
             if in_range(s - 4):
                 normalise(s - 4)
             if second_of_group(s - 6):
                 square_g((s - 6) // PAIRS_PER_GROUP)
             for i in store_now:
                 store_kv(i)
-
             if in_range(s - 1):
                 add_bias_k(s - 1)
             if 0 <= b < B and phase == 0:

@@ -30,6 +30,7 @@ E_BLOCKS = E // P
 
 RUN = 4
 ROUND_PARTS = 4
+G_PARTS = 8
 X_BUFS = 6
 NORM_STEP = PAIRS_PER_BATCH + 6
 K2_STRIDE = PAIRS_PER_GROUP
@@ -53,7 +54,7 @@ def tile_essattn_pa_t_kernel(tc, x, wk, bk, wv, bv, out_0, out_1):
         g_rows, gram, v_rows, v_grouped = {}, {}, {}, {}
         norm_sq, norm, r_norm, r_norm_rows = {}, {}, {}, {}
         v_codes, v_scales, k2_grouped, k2_codes, k2_scales, kv_ps = {}, {}, {}, {}, {}, {}
-        g_t, g_sq_sums = {}, {}
+        g_t, g_sq_sums, r_norm_sbuf = {}, {}, {}
 
         def load_x(j):
             if j >= PAIRS:
@@ -347,18 +348,24 @@ def tile_essattn_pa_t_kernel(tc, x, wk, bk, wv, bv, out_0, out_1):
                     stop=True,
                 )
 
-        def scale_k2(b, grp, engine, row):
+        def copy_norm(b):
+            r_norm_sbuf[b] = stream.tile([P, E], F32, name="r_norm_sbuf", tag="r_norm_sbuf")
+            nc.scalar.copy(out=r_norm_sbuf[b][:], in_=r_norm_rows[b][:])
+
+        def scale_k2(b, grp, engine, row, part=0, parts=1):
             i = b * GROUPS_PER_BATCH + grp
-            k2_grouped[i] = stream.tile(
-                [P, E, PACK], BF16, name="k2_grouped", tag="k2_grouped", bufs=4, align_bytes=64
-            )
+            if part == 0:
+                k2_grouped[i] = stream.tile(
+                    [P, E, PACK], BF16, name="k2_grouped", tag="k2_grouped", bufs=4, align_bytes=64
+                )
+            cols = slice(part * E // parts, (part + 1) * E // parts)
             engine.tensor_tensor(
-                out=k2_grouped[i][:].rearrange("p (c n) t -> p c t n", n=RUN),
-                in0=g_rows[i][:].rearrange("p t (c n) -> p c t n", n=RUN),
-                in1=row[:]
+                out=k2_grouped[i][:, cols, :].rearrange("p (c n) t -> p c t n", n=RUN),
+                in0=g_rows[i][:, :, cols].rearrange("p t (c n) -> p c t n", n=RUN),
+                in1=row[:, cols]
                 .rearrange("p (c n) -> p c n", n=RUN)
                 .unsqueeze(2)
-                .to_broadcast([P, E // RUN, PACK, RUN]),
+                .to_broadcast([P, E // RUN // parts, PACK, RUN]),
                 op=ALU.mult,
             )
 
@@ -407,20 +414,24 @@ def tile_essattn_pa_t_kernel(tc, x, wk, bk, wv, bv, out_0, out_1):
         k2_steps = {}
 
         def at(step, what, item):
-            k2_steps.setdefault(step, ([], [], [], []))[what].append(item)
+            k2_steps.setdefault(step, ([], [], [], [], []))[what].append(item)
 
         for b in range(B - 1):
+            start = NORM_STEP + b * PAIRS_PER_BATCH + 1
             for grp in range(GROUPS_PER_BATCH):
-                step = NORM_STEP + b * PAIRS_PER_BATCH + 1 + grp * K2_STRIDE
-                at(step, 0, b * GROUPS_PER_BATCH + grp)
+                step = start + grp * K2_STRIDE
+                if grp < GROUPS_PER_BATCH - 1:
+                    at(step, 0, b * GROUPS_PER_BATCH + grp)
                 at(step + 1, 1, b * GROUPS_PER_BATCH + grp)
+            for part in range(G_PARTS):
+                at(start + part, 4, (b, part))
             at(step + 1, 2, b)
             at(step + 2, 3, b)
 
         for s in range(-1, LAST_STEP + 1):
             v_now, v_one, v_two, v_three = (v_pair.get(s - d, -1) for d in range(4))
             b, phase = divmod(s - NORM_STEP, PAIRS_PER_BATCH)
-            scale_now, quantise_now, multiply_now, store_now = k2_steps.get(s, ([], [], [], []))
+            scale_now, quantise_now, multiply_now, store_now, share_now = k2_steps.get(s, ([], [], [], [], []))
 
             if in_range(s):
                 quantise_x(s)
@@ -452,6 +463,10 @@ def tile_essattn_pa_t_kernel(tc, x, wk, bk, wv, bv, out_0, out_1):
             if second_of_group(v_two):
                 for part in range(1, ROUND_PARTS):
                     round_v(v_two // PAIRS_PER_GROUP, part)
+            for b_k2, part in share_now:
+                scale_k2(
+                    b_k2, GROUPS_PER_BATCH - 1, nc.gpsimd, r_norm_sbuf[b_k2], part, G_PARTS
+                )
             if 0 <= b < B and phase == 0:
                 sum_norm(b)
             if 0 <= b < B and phase == 0:
@@ -469,6 +484,7 @@ def tile_essattn_pa_t_kernel(tc, x, wk, bk, wv, bv, out_0, out_1):
             if 0 <= b < B and phase == 0:
                 invert_norm(b)
                 spread_norm(b)
+                copy_norm(b)
             if in_range(s - 3):
                 invert_sum(s - 3)
             for i in quantise_now:
@@ -483,11 +499,9 @@ def tile_essattn_pa_t_kernel(tc, x, wk, bk, wv, bv, out_0, out_1):
 
         last = B - 1
         groups = range(GROUPS_PER_BATCH)
-        r_norm_sbuf = const.tile([P, E], F32)
-        nc.scalar.copy(out=r_norm_sbuf[:], in_=r_norm_rows[last][:])
         for grp in groups:
             if grp == GROUPS_PER_BATCH - 1:
-                scale_k2(last, grp, nc.gpsimd, r_norm_sbuf)
+                scale_k2(last, grp, nc.gpsimd, r_norm_sbuf[last])
             else:
                 scale_k2(last, grp, nc.vector, r_norm_rows[last])
         store_kv(last - 1)

@@ -32,7 +32,7 @@ RUN = 4
 ROUND_PARTS = 4
 G_PARTS = 8
 X_BUFS = 6
-NORM_STEP = PAIRS_PER_BATCH + 6
+NORM_STEP = PAIRS_PER_BATCH + 4
 K2_STRIDE = PAIRS_PER_GROUP
 LAST_STEP = NORM_STEP + (B - 1) * PAIRS_PER_BATCH
 X_CODE_BUFS = 6
@@ -395,11 +395,11 @@ def tile_essattn_pa_t_kernel(tc, x, wk, bk, wv, bv, out_0, out_1):
                 stop=(grp == GROUPS_PER_BATCH - 1),
             )
 
-        def multiply_kv(b):
-            kv_ps[b] = psum.tile([P, E_BLOCKS, E], F32, name="kv_ps", tag="v_acc", bufs=2)
-            for m in range(E_BLOCKS):
-                for grp in range(GROUPS_PER_BATCH):
-                    multiply_kv_group(b, grp, m, kv_ps[b][:, m, :])
+        def multiply_kv(b, m):
+            if m == 0:
+                kv_ps[b] = psum.tile([P, E_BLOCKS, E], F32, name="kv_ps", tag="v_acc", bufs=2)
+            for grp in range(GROUPS_PER_BATCH):
+                multiply_kv_group(b, grp, m, kv_ps[b][:, m, :])
 
         def store_kv(b):
             kv_rows = stream.tile([P, E_BLOCKS, E], F32, name="kv_rows", tag="kv_rows")
@@ -425,8 +425,9 @@ def tile_essattn_pa_t_kernel(tc, x, wk, bk, wv, bv, out_0, out_1):
                 at(step + 1, 1, b * GROUPS_PER_BATCH + grp)
             for part in range(G_PARTS):
                 at(start + part, 4, (b, part))
-            at(step + 1, 2, b)
-            at(step + 2, 3, b)
+            for m in range(E_BLOCKS):
+                at(step + 2 + m, 2, (b, m))
+            at(step + 4, 3, b)
 
         for s in range(-1, LAST_STEP + 1):
             v_now, v_one, v_two, v_three = (v_pair.get(s - d, -1) for d in range(4))
@@ -442,8 +443,8 @@ def tile_essattn_pa_t_kernel(tc, x, wk, bk, wv, bv, out_0, out_1):
             if in_range(s + 1):
                 transpose_x(s + 1)
             load_x(s + 1 + X_BUFS)
-            if second_of_group(s - 6):
-                transpose_g((s - 6) // PAIRS_PER_GROUP)
+            if second_of_group(s - 4):
+                transpose_g((s - 4) // PAIRS_PER_GROUP)
             if in_range(s):
                 project_k(s)
             if s == 0:
@@ -452,8 +453,10 @@ def tile_essattn_pa_t_kernel(tc, x, wk, bk, wv, bv, out_0, out_1):
                 quantise_w(1)
             if in_range(v_now):
                 project_v(v_now)
-            if in_range(s - 6):
-                multiply_g(s - 6)
+            for b_kv, m in multiply_now:
+                multiply_kv(b_kv, m)
+            if in_range(s - 4):
+                multiply_g(s - 4)
             if in_range(s - 2):
                 square_centred(s - 2)
                 add_eps(s - 2)
@@ -473,10 +476,10 @@ def tile_essattn_pa_t_kernel(tc, x, wk, bk, wv, bv, out_0, out_1):
                 root_norm(b)
             if in_range(s + 1):
                 regroup_x(s + 1)
-            if in_range(s - 4):
-                normalise(s - 4)
-            if second_of_group(s - 6):
-                square_g((s - 6) // PAIRS_PER_GROUP)
+            if in_range(s - 3):
+                normalise(s - 3)
+            if second_of_group(s - 4):
+                square_g((s - 4) // PAIRS_PER_GROUP)
             for i in store_now:
                 store_kv(i)
             if in_range(s - 1):
@@ -485,12 +488,10 @@ def tile_essattn_pa_t_kernel(tc, x, wk, bk, wv, bv, out_0, out_1):
                 invert_norm(b)
                 spread_norm(b)
                 copy_norm(b)
-            if in_range(s - 3):
-                invert_sum(s - 3)
+            if in_range(s - 2):
+                invert_sum(s - 2)
             for i in quantise_now:
                 quantise_k2(*divmod(i, GROUPS_PER_BATCH))
-            for i in multiply_now:
-                multiply_kv(i)
             if second_of_group(v_three):
                 quantise_v(v_three // PAIRS_PER_GROUP)
             for i in scale_now:
@@ -504,6 +505,8 @@ def tile_essattn_pa_t_kernel(tc, x, wk, bk, wv, bv, out_0, out_1):
                 scale_k2(last, grp, nc.gpsimd, r_norm_sbuf[last])
             else:
                 scale_k2(last, grp, nc.vector, r_norm_rows[last])
+        for m in range(E_BLOCKS):
+            multiply_kv(last - 1, m)
         store_kv(last - 1)
         kv_banks = [
             psum.tile([P, E], F32, name="kv_bank", tag=tag, bufs=2) for tag in ("v_acc", "k_acc")

from contextlib import ExitStack

import concourse.mybir as mybir
from concourse.masks import make_identity

F32 = mybir.dt.float32
BF16 = mybir.dt.bfloat16
U32 = mybir.dt.uint32
U8 = mybir.dt.uint8
FP8X4 = mybir.dt.float8_e4m3fn_x4
ALU = mybir.AluOpType
ACT = mybir.ActivationFunctionType

B, N, C, E = 4, 2048, 1024, 256
EPS_SUM = 1e-7
EPS_NORM = 1e-12
FLOPS = 2 * B * N * C * 2 * E + 2 * B * N * E * E

P = 128
PACK = 4
K_PASS = P * PACK
C_PASSES = C // K_PASS
WORDS = C // 2
PAIR = 2
PAIRS_PER_GROUP = PACK // PAIR
PAIRS_PER_BATCH = N // (PAIR * P)
GROUPS_PER_BATCH = N // K_PASS
PAIRS = B * PAIRS_PER_BATCH
E_BLOCKS = E // P

RUN = 4
ROUND_PARTS = 4
G_PARTS = 8
X_BUFS = 6
NORM_STEP = PAIRS_PER_BATCH + 4
K2_STRIDE = PAIRS_PER_GROUP
LAST_STEP = NORM_STEP + (B - 1) * PAIRS_PER_BATCH
X_CODE_BUFS = 6

def tile_essattn_pa_t_kernel(tc, x, wk, bk, wv, bv, out_0, out_1):
    nc = tc.nc
    x_groups = x.flatten_outer_dims().rearrange("(i p t) c -> i p t c", p=P, t=PACK)
    v_groups = out_1.flatten_outer_dims().rearrange("(i p t) e -> i p t e", p=P, t=PACK)

    with ExitStack() as ctx:
        ctx.enter_context(tc.manual_schedule())
        const = ctx.enter_context(tc.tile_pool(name="const", bufs=1))
        stream = ctx.enter_context(tc.tile_pool(name="stream", bufs=2))
        small = ctx.enter_context(tc.tile_pool(name="small", bufs=4))
        psum = ctx.enter_context(tc.psum_pool(name="psum", bufs=1))

        x_rows, x_t, x_grouped, x_codes, x_scales, k_acc, v_acc = {}, {}, {}, {}, {}, {}, {}
        kb, neg_mean, f, f_sum, f_sum_eps, r = {}, {}, {}, {}, {}, {}
        g_rows, gram, v_rows, v_grouped = {}, {}, {}, {}
        norm_sq, norm, r_norm, r_norm_rows = {}, {}, {}, {}
        v_codes, v_scales, k2_grouped, k2_codes, k2_scales, kv_ps = {}, {}, {}, {}, {}, {}
        g_t, g_sq_sums, r_norm_sbuf = {}, {}, {}

        def load_x(j):
            if j >= PAIRS:
                return
            i, h = divmod(j, PAIRS_PER_GROUP)
            x_rows[j] = stream.tile([P, PAIR * C], BF16, name="x_rows", tag="x_rows", bufs=X_BUFS)
            nc.sync.dma_start(
                out=x_rows[j][:].rearrange("p (t c) -> p t c", t=PAIR),
                in_=x_groups[i][:, h * PAIR : (h + 1) * PAIR, :],
            )

        ident = const.tile([P, P], F32)
        make_identity(nc, ident[:])

        one = const.tile([P, 1], F32)
        nc.vector.memset(one[:], 1.0)
        sqrt_one = const.tile([P, 1], F32)
        nc.scalar.sqrt(sqrt_one[:], one[:])

        bias_row = const.tile([P, 2 * E], BF16)
        nc.vector.memset(bias_row[:], 0.0)
        nc.sync.dma_start(out=bias_row[0:1, 0:E], in_=bk.unsqueeze(0))
        nc.sync.dma_start(out=bias_row[0:1, E : 2 * E], in_=bv.unsqueeze(0))
        ones = const.tile([P, P], BF16)
        nc.vector.memset(ones[:], 1.0)

        w_codes = const.tile([P, 2, C_PASSES, E], U32, align_bytes=64)
        w_scales = const.tile([P, 2, C_PASSES, E], U8, align_bytes=64)
        w_stage = ctx.enter_context(tc.tile_pool(name="w_stage", bufs=1))
        w_grouped = w_stage.tile([P, 2, C_PASSES, E, PACK], BF16, align_bytes=64)
        w_rows = []
        for side, w in enumerate((wk, wv)):
            rows = w_stage.tile([P, C_PASSES * PACK, E], BF16, name="w_rows", tag="w_rows", bufs=2)
            nc.sync.dma_start(
                out=rows[:].rearrange("p (h e) n -> p h (e n)", e=2),
                in_=w.rearrange("(h p e) n -> p h (e n)", p=P, e=2),
            )
            w_rows.append(rows)
            if side == 0:
                load_x(0)
        for j in range(1, X_BUFS):
            load_x(j)

        def regroup_w(side, c, copy):
            copy(
                out=w_grouped[:, side, c].rearrange("p (d n) t -> p d t n", n=RUN),
                in_=w_rows[side][:, c * PACK : (c + 1) * PACK, :].rearrange(
                    "p t (d n) -> p d t n", n=RUN
                ),
            )

        def quantise_w(side):
            nc.vector.quantize_mx(
                out=w_codes[:, side].rearrange("p c n -> p (c n)").bitcast(FP8X4),
                scales=w_scales[:, side].rearrange("p c n -> p (c n)"),
                in_=w_grouped[:, side].rearrange("p c n t -> p (c n t)"),
            )

        bias = const.tile([P, 2 * E], F32)
        bias_rows = psum.tile([P, 2 * E], F32, name="bias_rows", tag="gram")
        nc.tensor.matmul(out=bias_rows[:], lhsT=ones[:], rhs=bias_row[:], start=True, stop=True)
        nc.scalar.mul(bias[:, 0:E], bias_rows[:, 0:E], -1.0 / E)
        nc.scalar.copy(out=bias[:, E : 2 * E], in_=bias_rows[:, E : 2 * E])

        regroup_w(0, 0, nc.vector.tensor_copy)
        regroup_w(0, 1, nc.scalar.copy)
        quantise_w(0)

        masked = const.tile([P, P], F32)
        squares = const.tile([P, K_PASS], F32)

        def in_range(j):
            return 0 <= j < PAIRS

        def transpose_x(j):
            words = x_rows[j][:].bitcast(F32)
            x_t[j] = []
            for t in range(PAIR):
                bank = psum.tile([P, WORDS // P, P], F32, name="x_t", tag="x_t", bufs=PAIR)
                for q in range(WORDS // P):
                    first = t * WORDS + q * P
                    nc.tensor.transpose(bank[:, q, :], words[:, first : first + P], ident[:])
                x_t[j].append(bank)

        def regroup_x(j):
            x_grouped[j] = stream.tile(
                [P, PAIR * C], BF16, name="x_grouped", tag="x_grouped", align_bytes=64
            )
            words = x_grouped[j][:].bitcast(F32)
            for t in range(PAIR):
                nc.scalar.copy(
                    out=words[:, t * WORDS : (t + 1) * WORDS].rearrange(
                        "p (c r u) -> p c r u", c=C_PASSES, u=2
                    ),
                    in_=x_t[j][t][:].rearrange("p (c u) r -> p c r u", u=2),
                )

        def quantise_x(j):
            width = PAIR * C // PACK
            x_codes[j] = stream.tile(
                [P, width], U32, name="x_codes", tag="x_codes", bufs=X_CODE_BUFS, align_bytes=64
            )
            x_scales[j] = stream.tile(
                [P, width], U8, name="x_scales", tag="x_scales", bufs=X_CODE_BUFS, align_bytes=64
            )
            nc.vector.quantize_mx(
                out=x_codes[j][:].bitcast(FP8X4), scales=x_scales[j][:], in_=x_grouped[j][:]
            )

        def project(j, side, bank):
            for t in range(PAIR):
                for c in range(C_PASSES):
                    cols = slice((t * C_PASSES + c) * P, (t * C_PASSES + c + 1) * P)
                    nc.tensor.matmul_mx(
                        out=bank[:, t, :],
                        lhsT=x_codes[j][:, cols].bitcast(FP8X4),
                        lhsT_scale=x_scales[j][:, cols],
                        rhs=w_codes[:, side, c, :].bitcast(FP8X4),
                        rhs_scale=w_scales[:, side, c, :],
                        start=(c == 0),
                        stop=(c == C_PASSES - 1),
                    )

        def project_k(j):
            k_acc[j] = psum.tile([P, PAIR, E], F32, name="k_acc", tag="k_acc", bufs=2)
            project(j, 0, k_acc[j])

        def project_v(j):
            v_acc[j] = psum.tile([P, PAIR, E], F32, name="v_acc", tag="v_acc", bufs=2)
            project(j, 1, v_acc[j])

        def add_bias_k(j):
            kb[j] = stream.tile([P, PAIR, E], F32, name="kb", tag="kb")
            neg_mean[j] = small.tile([P, PAIR], F32, name="neg_mean", tag="neg_mean")
            for t in range(PAIR):
                nc.vector.scalar_tensor_tensor(
                    out=kb[j][:, t, :],
                    in0=k_acc[j][:, t, :],
                    scalar=-1.0 / E,
                    in1=bias[:, 0:E],
                    op0=ALU.mult,
                    op1=ALU.add,
                    accum_out=neg_mean[j][:, t : t + 1],
                )

        def add_bias_v(j):
            i, h = divmod(j, PAIRS_PER_GROUP)
            if h == 0:
                v_rows[i] = stream.tile([P, PACK, E], F32, name="v_rows", tag="v_rows", bufs=3)
            nc.vector.tensor_tensor(
                out=v_rows[i][:, h * PAIR : (h + 1) * PAIR, :],
                in0=v_acc[j][:],
                in1=bias[:, E : 2 * E].unsqueeze(1).to_broadcast([P, PAIR, E]),
                op=ALU.add,
            )

        def square_centred(j):
            f[j] = stream.tile([P, PAIR, E], F32, name="f", tag="f", bufs=3)
            f_sum[j] = small.tile([P, PAIR], F32, name="f_sum", tag="f_sum")
            for t in range(PAIR):
                nc.scalar.activation(
                    out=f[j][:, t, :],
                    in_=kb[j][:, t, :],
                    func=ACT.Square,
                    bias=neg_mean[j][:, t : t + 1],
                    scale=-float(E),
                    accum_out=f_sum[j][:, t : t + 1],
                )

        def add_eps(j):
            f_sum_eps[j] = small.tile([P, PAIR], F32, name="f_sum_eps", tag="f_sum_eps")
            nc.gpsimd.tensor_scalar(
                out=f_sum_eps[j][:], in0=f_sum[j][:], scalar1=EPS_SUM, scalar2=1.0,
                op0=ALU.add, op1=ALU.mult,
            )

        def invert_sum(j):
            r[j] = small.tile([P, PAIR], F32, name="r", tag="r")
            nc.vector.reciprocal(out=r[j][:], in_=f_sum_eps[j][:])

        def normalise(j):
            i, h = divmod(j, PAIRS_PER_GROUP)
            if h == 0:
                g_rows[i] = stream.tile([P, PACK, E], F32, name="g_rows", tag="g_rows", bufs=8)
            for t in range(PAIR):
                nc.scalar.activation(
                    out=g_rows[i][:, h * PAIR + t, :], in_=f[j][:, t, :], func=ACT.Copy,
                    scale=r[j][:, t : t + 1],
                )

        def multiply_g(j):
            i, h = divmod(j, PAIRS_PER_GROUP)
            b, part = divmod(j, PAIRS_PER_BATCH)
            if part == 0:
                gram[b] = psum.tile([P, P], F32, name="gram", tag="gram")
            for t in range(PAIR):
                block = g_rows[i][:, h * PAIR + t, 0:P]
                nc.tensor.matmul(
                    out=gram[b][:],
                    lhsT=block,
                    rhs=block,
                    start=(part == 0 and t == 0),
                    stop=(part == PAIRS_PER_BATCH - 1 and t == PAIR - 1),
                )

        def store_v(i):
            nc.sync.dma_start(out=v_groups[i], in_=v_rows[i][:])

        def round_v(i, part):
            if part == 0:
                v_grouped[i] = stream.tile(
                    [P, E, PACK], BF16, name="v_grouped", tag="v_grouped", align_bytes=64
                )
            cols = slice(part * E // ROUND_PARTS, (part + 1) * E // ROUND_PARTS)
            nc.gpsimd.tensor_scalar(
                out=v_grouped[i][:, cols, :].rearrange("p (c n) t -> p c t n", n=RUN),
                in0=v_rows[i][:, :, cols].rearrange("p t (c n) -> p c t n", n=RUN),
                scalar1=1.0,
                scalar2=0.0,
                op0=ALU.mult,
                op1=ALU.add,
            )

        def quantise_v(i):
            b, grp = divmod(i, GROUPS_PER_BATCH)
            if grp == 0:
                v_codes[b] = stream.tile(
                    [P, GROUPS_PER_BATCH, E], U32, name="v_codes", tag="v_codes", bufs=3,
                    align_bytes=64,
                )
                v_scales[b] = stream.tile(
                    [P, GROUPS_PER_BATCH, E], U8, name="v_scales", tag="v_scales", bufs=3,
                    align_bytes=64,
                )
            nc.vector.quantize_mx(
                out=v_codes[b][:, grp, :].bitcast(FP8X4),
                scales=v_scales[b][:, grp, :],
                in_=v_grouped[i][:].rearrange("p e t -> p (e t)"),
            )

        def transpose_g(i):
            g_t[i] = psum.tile([P, PACK, P], F32, name="g_t", tag="v_acc", bufs=2)
            for t in range(PACK):
                nc.tensor.transpose(g_t[i][:, t, :], g_rows[i][:, t, P:E], ident[:])

        def square_g(i):
            b, grp = divmod(i, GROUPS_PER_BATCH)
            if grp == 0:
                g_sq_sums[b] = small.tile(
                    [P, GROUPS_PER_BATCH], F32, name="g_sq_sums", tag="g_sq_sums"
                )
            nc.scalar.activation(
                out=squares[:],
                in_=g_t[i][:].rearrange("p t r -> p (t r)"),
                func=ACT.Square,
                accum_out=g_sq_sums[b][:, grp : grp + 1],
            )

        def sum_norm(b):
            norm_sq[b] = small.tile([P, E_BLOCKS], F32, name="norm_sq", tag="norm_sq")
            nc.vector.reduce_sum(
                out=norm_sq[b][:, 1:2], in_=g_sq_sums[b][:], axis=mybir.AxisListType.X
            )
            nc.vector.scalar_tensor_tensor(
                out=masked[:],
                in0=gram[b][:],
                scalar=1.0,
                in1=ident[:],
                op0=ALU.mult,
                op1=ALU.mult,
                accum_out=norm_sq[b][:, 0:1],
            )
            nc.vector.tensor_scalar_max(norm_sq[b][:], norm_sq[b][:], EPS_NORM * EPS_NORM)

        def root_norm(b):
            norm[b] = small.tile([P, E_BLOCKS], F32, name="norm", tag="norm")
            nc.scalar.sqrt(norm[b][:], norm_sq[b][:])

        def invert_norm(b):
            r_norm[b] = small.tile([P, E_BLOCKS], F32, name="r_norm", tag="r_norm")
            nc.vector.reciprocal(out=r_norm[b][:], in_=norm[b][:])

        def spread_norm(b):
            r_norm_rows[b] = psum.tile([P, E], F32, name="r_norm_rows", tag="r_norm_rows")
            for m in range(E_BLOCKS):
                nc.tensor.matmul(
                    out=r_norm_rows[b][:, m * P : (m + 1) * P],
                    lhsT=r_norm[b][:, m : m + 1].to_broadcast([P, P]),
                    rhs=ident[:],
                    start=True,
                    stop=True,
                )

        def copy_norm(b):
            r_norm_sbuf[b] = stream.tile([P, E], F32, name="r_norm_sbuf", tag="r_norm_sbuf")
            nc.scalar.copy(out=r_norm_sbuf[b][:], in_=r_norm_rows[b][:])

        def scale_k2(b, grp, engine, row, part=0, parts=1):
            i = b * GROUPS_PER_BATCH + grp
            if part == 0:
                k2_grouped[i] = stream.tile(
                    [P, E, PACK], BF16, name="k2_grouped", tag="k2_grouped", bufs=4, align_bytes=64
                )
            cols = slice(part * E // parts, (part + 1) * E // parts)
            engine.tensor_tensor(
                out=k2_grouped[i][:, cols, :].rearrange("p (c n) t -> p c t n", n=RUN),
                in0=g_rows[i][:, :, cols].rearrange("p t (c n) -> p c t n", n=RUN),
                in1=row[:, cols]
                .rearrange("p (c n) -> p c n", n=RUN)
                .unsqueeze(2)
                .to_broadcast([P, E // RUN // parts, PACK, RUN]),
                op=ALU.mult,
            )

        def quantise_k2(b, grp):
            i = b * GROUPS_PER_BATCH + grp
            if grp == 0:
                k2_codes[b] = stream.tile(
                    [P, GROUPS_PER_BATCH, E], U32, name="k2_codes", tag="k2_codes", align_bytes=64
                )
                k2_scales[b] = stream.tile(
                    [P, GROUPS_PER_BATCH, E], U8, name="k2_scales", tag="k2_scales", align_bytes=64
                )
            nc.vector.quantize_mx(
                out=k2_codes[b][:, grp, :].bitcast(FP8X4),
                scales=k2_scales[b][:, grp, :],
                in_=k2_grouped[i][:].rearrange("p e t -> p (e t)"),
            )

        def multiply_kv_group(b, grp, m, out):
            nc.tensor.matmul_mx(
                out=out,
                lhsT=k2_codes[b][:, grp, m * P : (m + 1) * P].bitcast(FP8X4),
                lhsT_scale=k2_scales[b][:, grp, m * P : (m + 1) * P],
                rhs=v_codes[b][:, grp, :].bitcast(FP8X4),
                rhs_scale=v_scales[b][:, grp, :],
                start=(grp == 0),
                stop=(grp == GROUPS_PER_BATCH - 1),
            )

        def multiply_kv(b, m):
            if m == 0:
                kv_ps[b] = psum.tile([P, E_BLOCKS, E], F32, name="kv_ps", tag="v_acc", bufs=2)
            for grp in range(GROUPS_PER_BATCH):
                multiply_kv_group(b, grp, m, kv_ps[b][:, m, :])

        def store_kv(b):
            kv_rows = stream.tile([P, E_BLOCKS, E], F32, name="kv_rows", tag="kv_rows")
            nc.scalar.copy(out=kv_rows[:], in_=kv_ps[b][:])
            nc.sync.dma_start(out=out_0[b].rearrange("(m p) e -> p m e", p=P), in_=kv_rows[:])

        def second_of_group(j):
            return in_range(j) and j % PAIRS_PER_GROUP == PAIRS_PER_GROUP - 1

        v_pair = {j: j for j in range(PAIRS)}

        k2_steps = {}

        def at(step, what, item):
            k2_steps.setdefault(step, ([], [], [], [], []))[what].append(item)

        for b in range(B - 1):
            start = NORM_STEP + b * PAIRS_PER_BATCH + 1
            for grp in range(GROUPS_PER_BATCH):
                step = start + grp * K2_STRIDE
                if grp < GROUPS_PER_BATCH - 1:
                    at(step, 0, b * GROUPS_PER_BATCH + grp)
                at(step + 1, 1, b * GROUPS_PER_BATCH + grp)
            for part in range(G_PARTS):
                at(start + part, 4, (b, part))
            for m in range(E_BLOCKS):
                at(step + 2 + m, 2, (b, m))
            at(step + 4, 3, b)

        for s in range(-1, LAST_STEP + 1):
            v_now, v_one, v_two, v_three = (v_pair.get(s - d, -1) for d in range(4))
            b, phase = divmod(s - NORM_STEP, PAIRS_PER_BATCH)
            scale_now, quantise_now, multiply_now, store_now, share_now = k2_steps.get(s, ([], [], [], [], []))

            if in_range(s):
                quantise_x(s)
            if in_range(v_one):
                add_bias_v(v_one)
            if second_of_group(v_one):
                store_v(v_one // PAIRS_PER_GROUP)
            if in_range(s + 1):
                transpose_x(s + 1)
            load_x(s + 1 + X_BUFS)
            if second_of_group(s - 4):
                transpose_g((s - 4) // PAIRS_PER_GROUP)
            if in_range(s):
                project_k(s)
            if s == 0:
                regroup_w(1, 0, nc.vector.tensor_copy)
                regroup_w(1, 1, nc.scalar.copy)
                quantise_w(1)
            if in_range(v_now):
                project_v(v_now)
            for b_kv, m in multiply_now:
                multiply_kv(b_kv, m)
            if in_range(s - 4):
                multiply_g(s - 4)
            if in_range(s - 2):
                square_centred(s - 2)
                add_eps(s - 2)
            if second_of_group(v_one):
                for part in range(1):
                    round_v(v_one // PAIRS_PER_GROUP, part)
            if second_of_group(v_two):
                for part in range(1, ROUND_PARTS):
                    round_v(v_two // PAIRS_PER_GROUP, part)
            for b_k2, part in share_now:
                scale_k2(
                    b_k2, GROUPS_PER_BATCH - 1, nc.gpsimd, r_norm_sbuf[b_k2], part, G_PARTS
                )
            if 0 <= b < B and phase == 0:
                sum_norm(b)
            if 0 <= b < B and phase == 0:
                root_norm(b)
            if in_range(s + 1):
                regroup_x(s + 1)
            if in_range(s - 3):
                normalise(s - 3)
            if second_of_group(s - 4):
                square_g((s - 4) // PAIRS_PER_GROUP)
            for i in store_now:
                store_kv(i)
            if in_range(s - 1):
                add_bias_k(s - 1)
            if 0 <= b < B and phase == 0:
                invert_norm(b)
                spread_norm(b)
                copy_norm(b)
            if in_range(s - 2):
                invert_sum(s - 2)
            for i in quantise_now:
                quantise_k2(*divmod(i, GROUPS_PER_BATCH))
            if second_of_group(v_three):
                quantise_v(v_three // PAIRS_PER_GROUP)
            for i in scale_now:
                b_k2, grp = divmod(i, GROUPS_PER_BATCH)
                scale_k2(b_k2, grp, nc.vector, r_norm_rows[b_k2])

        last = B - 1
        groups = range(GROUPS_PER_BATCH)
        for grp in groups:
            if grp == GROUPS_PER_BATCH - 1:
                scale_k2(last, grp, nc.gpsimd, r_norm_sbuf[last])
            else:
                scale_k2(last, grp, nc.vector, r_norm_rows[last])
        for m in range(E_BLOCKS):
            multiply_kv(last - 1, m)
        store_kv(last - 1)
        kv_banks = [
            psum.tile([P, E], F32, name="kv_bank", tag=tag, bufs=2) for tag in ("v_acc", "k_acc")
        ]
        for grp in groups:
            quantise_k2(last, grp)
            for m, bank in enumerate(kv_banks):
                multiply_kv_group(last, grp, m, bank[:])
        for bank, m, copy, queue in (
            (kv_banks[0], 0, nc.scalar.copy, nc.sync),
            (kv_banks[1], 1, nc.vector.tensor_copy, nc.scalar),
        ):
            rows = stream.tile([P, E], F32, name="kv_block", tag="kv_block")
            copy(out=rows[:], in_=bank[:])
            queue.dma_start(out=out_0[last][m * P : (m + 1) * P, :], in_=rows[:])
